import numpy as np
import ml_dtypes


def mxq(x, axis, fmt="e4m3"):
    dtype, down = {"e4m3": (ml_dtypes.float8_e4m3fn, 7), "e5m2": (ml_dtypes.float8_e5m2, 14)}[fmt]
    v = np.moveaxis(np.asarray(x, np.float32).astype(ml_dtypes.bfloat16).astype(np.float64), axis, -1)
    blocks = v.reshape(v.shape[:-1] + (-1, 32))
    amax = np.abs(blocks).max(-1, keepdims=True)
    byte = np.maximum(np.where(amax > 0, np.frexp(amax)[1] - 1 + 127, 0) - down, 1)
    scale = np.exp2(byte - 127.0)
    codes = (blocks / scale).astype(np.float32).astype(dtype).astype(np.float64)
    return np.moveaxis((codes * scale).reshape(v.shape), -1, axis)


WIDE = False


def mx_kscale(k):
    if not WIDE:
        return np.ones(k)
    levels = np.array([10, -10, 5, -5, 0])
    a = np.random.permutation(np.resize(levels, k // 512 * 4)).reshape(k // 512, 4)
    idx = np.arange(k)
    return np.exp2(a[idx // 512, idx % 128 // 32])


BF16 = ml_dtypes.bfloat16


def bf(x):
    return np.asarray(x, np.float32).astype(BF16)


def f64(x):
    return np.asarray(x).astype(np.float64)


B, IN, OUT, G, SH = 1024, 1024, 1024, 3, 512
BASIS_EPS = 1e-6


def setup_inputs():
    s = mx_kscale(IN)
    return {"x": bf(np.random.standard_normal((B, IN)) * s),
            "base_weight": bf(np.random.standard_normal((OUT, IN)) * 0.7 / np.sqrt(IN) / s[None, :]),
            "spline_weight": bf(np.random.standard_normal((OUT, IN, G)) * 0.7 / np.sqrt(IN))}


def reference(x, base_weight, spline_weight):
    x = f64(x)
    base_out = mxq(x, 1, "e4m3") @ mxq(f64(base_weight), 1, "e4m3").T
    grid = np.linspace(-1.0, 1.0, G)
    d = np.abs(x[..., None] - grid)
    basis = np.where(d < 1.0, (1.0 - d) ** 2, 0.0)
    basis = basis / (basis.sum(axis=-1, keepdims=True) + BASIS_EPS)
    bas = basis.transpose(0, 2, 1).reshape(B, G * IN)
    ws = f64(spline_weight).transpose(0, 2, 1).reshape(OUT, G * IN)
    spline_out = mxq(bas, 1, "e4m3") @ mxq(ws, 1, "e4m3").T
    return base_out + spline_out

@@ -1,0 +1,254 @@
+from contextlib import ExitStack
+
+import concourse.mybir as mybir
+from concourse.masks import make_identity
+
+BF16 = mybir.dt.bfloat16
+F32 = mybir.dt.float32
+U32 = mybir.dt.uint32
+U8 = mybir.dt.uint8
+I32 = mybir.dt.int32
+FP8X4 = mybir.dt.float8_e4m3fn_x4
+ACT = mybir.ActivationFunctionType
+ALU = mybir.AluOpType
+
+P = 128
+PACK = 4
+ROWS = 1024
+FEATURES = 1024
+GRID = 3
+BASIS_EPS = 1e-6
+
+ROW_TILES = ROWS // P
+WORD_BLOCKS = FEATURES // 2 // P
+MATRIX_PASSES = FEATURES // (P * PACK)
+MATRICES = 1 + GRID
+PASSES = MATRICES * MATRIX_PASSES
+PASS_COLS = P * PACK
+TILE_COLS = MATRIX_PASSES * PASS_COLS
+N_TILE = 512
+N_TILES = ROWS // N_TILE
+
+GRID_ORDER = (1, 2, 0)
+
+FLOPS = 2 * ROWS * ROWS * FEATURES * MATRICES
+
+CLEAR_SIGNS = 0x7FFF7FFF
+
+LOAD_AHEAD = 2
+WEIGHT_LAG = 2
+BASIS_SHIFT = ROW_TILES - 1 + WEIGHT_LAG
+STEPS = BASIS_SHIFT + ROW_TILES + 1
+LOG_GROUP = 2
+
+
+def tile_kanlayer_pa_kernel(tc, x, base_weight, spline_weight, out):
+    nc = tc.nc
+    with ExitStack() as ctx:
+        consts = ctx.enter_context(tc.tile_pool(name="consts", bufs=1))
+        keep = ctx.enter_context(tc.tile_pool(name="keep", bufs=1))
+        loads = ctx.enter_context(tc.tile_pool(name="loads", bufs=LOAD_AHEAD + 1))
+        prep = ctx.enter_context(tc.tile_pool(name="prep", bufs=2))
+        work = ctx.enter_context(tc.tile_pool(name="work", bufs=2))
+        psum = ctx.enter_context(tc.psum_pool(name="psum", bufs=8))
+
+        ident = consts.tile([P, P], F32)
+        make_identity(nc, ident[:])
+        one_col = consts.tile([P, 1], F32)
+        nc.vector.memset(one_col[:], 1.0)
+        eps_col = consts.tile([P, 1], F32)
+        nc.vector.memset(eps_col[:], BASIS_EPS)
+
+        x_grouped = keep.tile([P, ROW_TILES * TILE_COLS], BF16, align_bytes=64)
+        x_grouped_words = x_grouped[:].bitcast(F32)
+        x_grouped_bits = x_grouped[:].bitcast(I32)
+        w_codes = keep.tile([P, PASSES, ROWS], U32, align_bytes=64)
+        w_scales = keep.tile([P, PASSES, ROWS], U8, align_bytes=64)
+
+        natural = {}
+        grouped_weights = {}
+        hats = {}
+        squares = {}
+        normaliser = {}
+        basis = {}
+        quantised = {}
+        sums = {}
+
+        def in_range(j):
+            return 0 <= j < ROW_TILES
+
+        def load_row_tile(r):
+            rows = slice(r * P, (r + 1) * P)
+            sw_nat = loads.tile([P, FEATURES * GRID], BF16)
+            nc.sync.dma_start(out=sw_nat[:], in_=spline_weight[rows, :, :].rearrange("o i g -> o (i g)"))
+            x_nat = loads.tile([P, FEATURES], BF16)
+            nc.sync.dma_start(out=x_nat[:], in_=x[rows, :])
+            bw_nat = loads.tile([P, FEATURES], BF16)
+            nc.sync.dma_start(out=bw_nat[:], in_=base_weight[rows, :])
+            natural[r] = (x_nat, bw_nat, sw_nat)
+
+        def transpose_row_tile(natural_words, grouped_words):
+            bank = psum.tile([P, WORD_BLOCKS, P], F32, tag="bank")
+            for w in range(WORD_BLOCKS):
+                nc.tensor.transpose(bank[:, w, :], natural_words[:, w * P : (w + 1) * P], ident[:])
+            nc.scalar.copy(
+                out=grouped_words.rearrange("p (c r u) -> p c r u", c=MATRIX_PASSES, u=2),
+                in_=bank[:].rearrange("p (c u) r -> p c r u", u=2),
+            )
+
+        def prepare_row_tile(r):
+            x_nat, bw_nat, sw_nat = natural[r]
+            words = TILE_COLS // 2
+            w_grouped = prep.tile([P, MATRICES * TILE_COLS], BF16, bufs=WEIGHT_LAG + 1, align_bytes=64)
+            w_grouped_words = w_grouped[:].bitcast(F32)
+            transpose_row_tile(x_nat[:].bitcast(F32), x_grouped_words[:, r * words : (r + 1) * words])
+            transpose_row_tile(bw_nat[:].bitcast(F32), w_grouped_words[:, 0:words])
+            sorted_sw = prep.tile([P, GRID * FEATURES], BF16)
+            sorted_words = sorted_sw[:].bitcast(F32)
+            by_grid = sw_nat[:].rearrange("p (i g) -> p g i", g=GRID)
+            for n, g in enumerate(GRID_ORDER):
+                nc.vector.tensor_copy(out=sorted_sw[:, n * FEATURES : (n + 1) * FEATURES], in_=by_grid[:, g, :])
+                transpose_row_tile(
+                    sorted_words[:, n * words : (n + 1) * words],
+                    w_grouped_words[:, (1 + n) * words : (2 + n) * words],
+                )
+            grouped_weights[r] = w_grouped
+
+        def quantise_weights(r):
+            w_grouped = grouped_weights[r]
+            cols = slice(r * P, (r + 1) * P)
+            for k in range(PASSES):
+                nc.vector.quantize_mx(
+                    out=w_codes[:, k, cols].bitcast(FP8X4),
+                    scales=w_scales[:, k, cols],
+                    in_=w_grouped[:, k * PASS_COLS : (k + 1) * PASS_COLS],
+                )
+
+        def make_hats(j):
+            words = TILE_COLS // 2
+            a = work.tile([P, TILE_COLS], BF16, bufs=1)
+            nc.vector.tensor_single_scalar(
+                out=a[:].bitcast(I32),
+                in_=x_grouped_bits[:, j * words : (j + 1) * words],
+                scalar=CLEAR_SIGNS,
+                op=ALU.bitwise_and,
+            )
+            twice_min1 = work.tile([P, TILE_COLS], BF16)
+            nc.vector.tensor_scalar(out=twice_min1[:], in0=a[:], scalar1=1.0, scalar2=2.0, op0=ALU.min, op1=ALU.mult)
+            min2 = work.tile([P, TILE_COLS], BF16, bufs=1)
+            nc.vector.tensor_single_scalar(out=min2[:], in_=a[:], scalar=2.0, op=ALU.min)
+            side = work.tile([P, TILE_COLS], BF16)
+            nc.vector.tensor_tensor(out=side[:], in0=twice_min1[:], in1=min2[:], op=ALU.subtract)
+            hats[j] = (twice_min1, side)
+
+        def square_hats(j):
+            twice_min1, side = hats[j]
+            r_side = work.tile([P, TILE_COLS], F32, bufs=LOG_GROUP + 2)
+            nc.scalar.activation(out=r_side[:], in_=side[:], func=ACT.Square)
+            r_centre = work.tile([P, TILE_COLS], F32, bufs=LOG_GROUP + 2)
+            nc.scalar.activation(out=r_centre[:], in_=twice_min1[:], func=ACT.Square, scale=-0.5, bias=one_col[:])
+            squares[j] = (r_side, r_centre)
+
+        def add_squares(j):
+            r_side, r_centre = squares[j]
+            norm = work.tile([P, TILE_COLS], F32, bufs=LOG_GROUP + 1)
+            nc.vector.tensor_tensor(out=norm[:], in0=r_side[:], in1=r_centre[:], op=ALU.add)
+            normaliser[j] = norm
+
+        def take_log(j):
+            norm = normaliser[j]
+            nc.scalar.activation(out=norm[:], in_=norm[:], func=ACT.Ln, bias=eps_col[:])
+
+        def take_exp(j):
+            norm = normaliser[j]
+            nc.scalar.activation(out=norm[:], in_=norm[:], func=ACT.Exp, scale=-1.0)
+
+        def make_basis(j):
+            r_side, r_centre = squares[j]
+            norm = normaliser[j]
+            x_tile = x_grouped[:, j * TILE_COLS : (j + 1) * TILE_COLS]
+            planes = work.tile([P, GRID * TILE_COLS], BF16, align_bytes=64)
+            centre = planes[:, 0:TILE_COLS]
+            right = planes[:, TILE_COLS : 2 * TILE_COLS]
+            left = planes[:, 2 * TILE_COLS : 3 * TILE_COLS]
+            b_side = work.tile([P, TILE_COLS], BF16, bufs=1)
+            nc.vector.tensor_tensor(out=b_side[:], in0=r_side[:], in1=norm[:], op=ALU.mult)
+            nc.vector.tensor_tensor(out=centre, in0=r_centre[:], in1=norm[:], op=ALU.mult)
+            positive = work.tile([P, TILE_COLS], BF16, bufs=1)
+            nc.vector.tensor_single_scalar(out=positive[:], in_=x_tile, scalar=0.0, op=ALU.is_gt)
+            nc.vector.tensor_tensor(out=right, in0=b_side[:], in1=positive[:], op=ALU.mult)
+            nc.vector.tensor_tensor(out=left, in0=b_side[:], in1=right, op=ALU.subtract)
+            basis[j] = planes
+
+        def quantise_batch_tile(j):
+            planes = basis[j]
+            codes = work.tile([P, PASSES * P], U32, bufs=3, align_bytes=64)
+            scales = work.tile([P, PASSES * P], U8, bufs=3, align_bytes=64)
+            width = MATRIX_PASSES * P
+            sources = [x_grouped[:, j * TILE_COLS : (j + 1) * TILE_COLS]]
+            sources.extend(planes[:, n * TILE_COLS : (n + 1) * TILE_COLS] for n in range(GRID))
+            for n, source in enumerate(sources):
+                nc.vector.quantize_mx(
+                    out=codes[:, n * width : (n + 1) * width].bitcast(FP8X4),
+                    scales=scales[:, n * width : (n + 1) * width],
+                    in_=source,
+                )
+            quantised[j] = (codes, scales)
+
+        def multiply(j):
+            codes, scales = quantised[j]
+            banks = []
+            for n in range(N_TILES):
+                acc = psum.tile([P, N_TILE], F32, tag="bank")
+                banks.append(acc)
+            for k in range(PASSES):
+                rows = slice(k * P, (k + 1) * P)
+                for n in range(N_TILES):
+                    cols = slice(n * N_TILE, (n + 1) * N_TILE)
+                    nc.tensor.matmul_mx(
+                        out=banks[n][:],
+                        lhsT=codes[:, rows].bitcast(FP8X4),
+                        lhsT_scale=scales[:, rows],
+                        rhs=w_codes[:, k, cols].bitcast(FP8X4),
+                        rhs_scale=w_scales[:, k, cols],
+                        start=(k == 0),
+                        stop=(k == PASSES - 1),
+                    )
+            sums[j] = banks
+
+        def store(j):
+            for n, acc in enumerate(sums[j]):
+                result = work.tile([P, N_TILE], F32, bufs=4)
+                nc.scalar.copy(out=result[:], in_=acc[:])
+                nc.sync.dma_start(out=out[j * P : (j + 1) * P, n * N_TILE : (n + 1) * N_TILE], in_=result[:])
+
+        with tc.manual_schedule():
+            for r in range(LOAD_AHEAD):
+                load_row_tile(r)
+            for step in range(STEPS):
+                if in_range(step + LOAD_AHEAD):
+                    load_row_tile(step + LOAD_AHEAD)
+                if in_range(step):
+                    prepare_row_tile(step)
+                if in_range(step - WEIGHT_LAG):
+                    quantise_weights(step - WEIGHT_LAG)
+                j = step - BASIS_SHIFT
+                newest = j + LOG_GROUP
+                if in_range(newest):
+                    add_squares(newest)
+                if in_range(newest + 1):
+                    square_hats(newest + 1)
+                if in_range(newest):
+                    take_log(newest)
+                    if newest % LOG_GROUP == LOG_GROUP - 1:
+                        for member in range(newest - LOG_GROUP + 1, newest + 1):
+                            take_exp(member)
+                if in_range(j):
+                    make_basis(j)
+                if in_range(newest + 2):
+                    make_hats(newest + 2)
+                if in_range(j):
+                    quantise_batch_tile(j)
+                    multiply(j)
+                if in_range(j - 1):
+                    store(j - 1)

@@ -30,6 +30,9 @@ N_TILE = 512
 N_TILES = ROWS // N_TILE
 
 GRID_ORDER = (1, 2, 0)
+CENTRE = 0
+RIGHT = 1
+LEFT = 2
 
 FLOPS = 2 * ROWS * ROWS * FEATURES * MATRICES
 
@@ -39,7 +42,7 @@ LOAD_AHEAD = 2
 WEIGHT_LAG = 2
 BASIS_SHIFT = ROW_TILES - 1 + WEIGHT_LAG
 STEPS = BASIS_SHIFT + ROW_TILES + 1
-LOG_GROUP = 2
+LOG_GROUP = 4
 
 
 def tile_kanlayer_pa_kernel(tc, x, base_weight, spline_weight, out):
@@ -67,7 +70,12 @@ def tile_kanlayer_pa_kernel(tc, x, base_weight, spline_weight, out):
 
         natural = {}
         grouped_weights = {}
-        hats = {}
+        abs_x = {}
+        clamped_one = {}
+        clamped_two = {}
+        side_hat = {}
+        is_positive = {}
+        side_basis = {}
         squares = {}
         normaliser = {}
         basis = {}
@@ -124,7 +132,10 @@ def tile_kanlayer_pa_kernel(tc, x, base_weight, spline_weight, out):
                     in_=w_grouped[:, k * PASS_COLS : (k + 1) * PASS_COLS],
                 )
 
-        def make_hats(j):
+        def x_tile(j):
+            return x_grouped[:, j * TILE_COLS : (j + 1) * TILE_COLS]
+
+        def take_abs(j):
             words = TILE_COLS // 2
             a = work.tile([P, TILE_COLS], BF16, bufs=1)
             nc.vector.tensor_single_scalar(
@@ -133,20 +144,30 @@ def tile_kanlayer_pa_kernel(tc, x, base_weight, spline_weight, out):
                 scalar=CLEAR_SIGNS,
                 op=ALU.bitwise_and,
             )
+            abs_x[j] = a
+
+        def clamp_at_one(j):
             twice_min1 = work.tile([P, TILE_COLS], BF16)
-            nc.vector.tensor_scalar(out=twice_min1[:], in0=a[:], scalar1=1.0, scalar2=2.0, op0=ALU.min, op1=ALU.mult)
+            nc.vector.tensor_scalar(
+                out=twice_min1[:], in0=abs_x[j][:], scalar1=1.0, scalar2=2.0, op0=ALU.min, op1=ALU.mult
+            )
+            clamped_one[j] = twice_min1
+
+        def clamp_at_two(j):
             min2 = work.tile([P, TILE_COLS], BF16, bufs=1)
-            nc.vector.tensor_single_scalar(out=min2[:], in_=a[:], scalar=2.0, op=ALU.min)
+            nc.vector.tensor_single_scalar(out=min2[:], in_=abs_x[j][:], scalar=2.0, op=ALU.min)
+            clamped_two[j] = min2
+
+        def make_side_hat(j):
             side = work.tile([P, TILE_COLS], BF16)
-            nc.vector.tensor_tensor(out=side[:], in0=twice_min1[:], in1=min2[:], op=ALU.subtract)
-            hats[j] = (twice_min1, side)
+            nc.vector.tensor_tensor(out=side[:], in0=clamped_one[j][:], in1=clamped_two[j][:], op=ALU.subtract)
+            side_hat[j] = side
 
         def square_hats(j):
-            twice_min1, side = hats[j]
             r_side = work.tile([P, TILE_COLS], F32, bufs=LOG_GROUP + 2)
-            nc.scalar.activation(out=r_side[:], in_=side[:], func=ACT.Square)
+            nc.scalar.activation(out=r_side[:], in_=side_hat[j][:], func=ACT.Square)
             r_centre = work.tile([P, TILE_COLS], F32, bufs=LOG_GROUP + 2)
-            nc.scalar.activation(out=r_centre[:], in_=twice_min1[:], func=ACT.Square, scale=-0.5, bias=one_col[:])
+            nc.scalar.activation(out=r_centre[:], in_=clamped_one[j][:], func=ACT.Square, scale=-0.5, bias=one_col[:])
             squares[j] = (r_side, r_centre)
 
         def add_squares(j):
@@ -163,37 +184,53 @@ def tile_kanlayer_pa_kernel(tc, x, base_weight, spline_weight, out):
             norm = normaliser[j]
             nc.scalar.activation(out=norm[:], in_=norm[:], func=ACT.Exp, scale=-1.0)
 
-        def make_basis(j):
-            r_side, r_centre = squares[j]
-            norm = normaliser[j]
-            x_tile = x_grouped[:, j * TILE_COLS : (j + 1) * TILE_COLS]
-            planes = work.tile([P, GRID * TILE_COLS], BF16, align_bytes=64)
-            centre = planes[:, 0:TILE_COLS]
-            right = planes[:, TILE_COLS : 2 * TILE_COLS]
-            left = planes[:, 2 * TILE_COLS : 3 * TILE_COLS]
-            b_side = work.tile([P, TILE_COLS], BF16, bufs=1)
-            nc.vector.tensor_tensor(out=b_side[:], in0=r_side[:], in1=norm[:], op=ALU.mult)
-            nc.vector.tensor_tensor(out=centre, in0=r_centre[:], in1=norm[:], op=ALU.mult)
+        def mark_positive(j):
             positive = work.tile([P, TILE_COLS], BF16, bufs=1)
-            nc.vector.tensor_single_scalar(out=positive[:], in_=x_tile, scalar=0.0, op=ALU.is_gt)
-            nc.vector.tensor_tensor(out=right, in0=b_side[:], in1=positive[:], op=ALU.mult)
-            nc.vector.tensor_tensor(out=left, in0=b_side[:], in1=right, op=ALU.subtract)
-            basis[j] = planes
+            nc.vector.tensor_single_scalar(out=positive[:], in_=x_tile(j), scalar=0.0, op=ALU.is_gt)
+            is_positive[j] = positive
 
-        def quantise_batch_tile(j):
-            planes = basis[j]
-            codes = work.tile([P, PASSES * P], U32, bufs=3, align_bytes=64)
-            scales = work.tile([P, PASSES * P], U8, bufs=3, align_bytes=64)
+        def scale_side(j):
+            b_side = work.tile([P, TILE_COLS], BF16, bufs=1)
+            nc.vector.tensor_tensor(out=b_side[:], in0=squares[j][0][:], in1=normaliser[j][:], op=ALU.mult)
+            side_basis[j] = b_side
+
+        def plane(j, n):
+            return basis[j][:, n * TILE_COLS : (n + 1) * TILE_COLS]
+
+        def scale_centre(j):
+            planes = work.tile([P, GRID * TILE_COLS], BF16, bufs=1, align_bytes=64)
+            basis[j] = planes
+            nc.vector.tensor_tensor(out=plane(j, CENTRE), in0=squares[j][1][:], in1=normaliser[j][:], op=ALU.mult)
+
+        def keep_right(j):
+            nc.vector.tensor_tensor(out=plane(j, RIGHT), in0=side_basis[j][:], in1=is_positive[j][:], op=ALU.mult)
+
+        def keep_left(j):
+            nc.vector.tensor_tensor(out=plane(j, LEFT), in0=side_basis[j][:], in1=plane(j, RIGHT), op=ALU.subtract)
+
+        def quantise_matrix(j, m, source):
+            codes, scales = quantised[j]
             width = MATRIX_PASSES * P
-            sources = [x_grouped[:, j * TILE_COLS : (j + 1) * TILE_COLS]]
-            sources.extend(planes[:, n * TILE_COLS : (n + 1) * TILE_COLS] for n in range(GRID))
-            for n, source in enumerate(sources):
-                nc.vector.quantize_mx(
-                    out=codes[:, n * width : (n + 1) * width].bitcast(FP8X4),
-                    scales=scales[:, n * width : (n + 1) * width],
-                    in_=source,
-                )
+            nc.vector.quantize_mx(
+                out=codes[:, m * width : (m + 1) * width].bitcast(FP8X4),
+                scales=scales[:, m * width : (m + 1) * width],
+                in_=source,
+            )
+
+        def quantise_x(j):
+            codes = work.tile([P, PASSES * P], U32, align_bytes=64)
+            scales = work.tile([P, PASSES * P], U8, align_bytes=64)
             quantised[j] = (codes, scales)
+            quantise_matrix(j, 0, x_tile(j))
+
+        def quantise_centre(j):
+            quantise_matrix(j, 1 + CENTRE, plane(j, CENTRE))
+
+        def quantise_right(j):
+            quantise_matrix(j, 1 + RIGHT, plane(j, RIGHT))
+
+        def quantise_left(j):
+            quantise_matrix(j, 1 + LEFT, plane(j, LEFT))
 
         def multiply(j):
             codes, scales = quantised[j]
@@ -218,37 +255,42 @@ def tile_kanlayer_pa_kernel(tc, x, base_weight, spline_weight, out):
 
         def store(j):
             for n, acc in enumerate(sums[j]):
-                result = work.tile([P, N_TILE], F32, bufs=4)
+                result = work.tile([P, N_TILE], F32, bufs=3)
                 nc.scalar.copy(out=result[:], in_=acc[:])
                 nc.sync.dma_start(out=out[j * P : (j + 1) * P, n * N_TILE : (n + 1) * N_TILE], in_=result[:])
+
+        def run(stage, j):
+            if in_range(j):
+                stage(j)
 
         with tc.manual_schedule():
             for r in range(LOAD_AHEAD):
                 load_row_tile(r)
             for step in range(STEPS):
-                if in_range(step + LOAD_AHEAD):
-                    load_row_tile(step + LOAD_AHEAD)
-                if in_range(step):
-                    prepare_row_tile(step)
-                if in_range(step - WEIGHT_LAG):
-                    quantise_weights(step - WEIGHT_LAG)
-                j = step - BASIS_SHIFT
-                newest = j + LOG_GROUP
-                if in_range(newest):
-                    add_squares(newest)
-                if in_range(newest + 1):
-                    square_hats(newest + 1)
-                if in_range(newest):
-                    take_log(newest)
-                    if newest % LOG_GROUP == LOG_GROUP - 1:
-                        for member in range(newest - LOG_GROUP + 1, newest + 1):
-                            take_exp(member)
-                if in_range(j):
-                    make_basis(j)
-                if in_range(newest + 2):
-                    make_hats(newest + 2)
-                if in_range(j):
-                    quantise_batch_tile(j)
-                    multiply(j)
-                if in_range(j - 1):
-                    store(j - 1)
+                run(load_row_tile, step + LOAD_AHEAD)
+                run(prepare_row_tile, step)
+                run(quantise_weights, step - WEIGHT_LAG)
+                done = step - BASIS_SHIFT
+                summed = done + LOG_GROUP
+                begun = summed + 2
+                run(mark_positive, done)
+                run(take_abs, begun)
+                run(add_squares, summed)
+                run(square_hats, summed + 1)
+                run(take_log, summed)
+                if in_range(summed) and summed % LOG_GROUP == LOG_GROUP - 1:
+                    for member in range(summed - LOG_GROUP + 1, summed + 1):
+                        take_exp(member)
+                run(clamp_at_one, begun)
+                run(scale_side, done)
+                run(clamp_at_two, begun)
+                run(scale_centre, done)
+                run(make_side_hat, begun)
+                run(keep_right, done)
+                run(quantise_x, done)
+                run(keep_left, done)
+                run(quantise_centre, done)
+                run(quantise_right, done)
+                run(quantise_left, done)
+                run(multiply, done)
+                run(store, done - 1)

@@ -53,10 +53,16 @@ def tile_kanlayer_pa_kernel(tc, x, base_weight, spline_weight, out):
         loads = ctx.enter_context(tc.tile_pool(name="loads", bufs=LOAD_AHEAD + 1))
         prep = ctx.enter_context(tc.tile_pool(name="prep", bufs=2))
         work = ctx.enter_context(tc.tile_pool(name="work", bufs=2))
-        psum = ctx.enter_context(tc.psum_pool(name="psum", bufs=8))
+        psum = ctx.enter_context(tc.psum_pool(name="psum", bufs=2))
 
         ident = consts.tile([P, P], F32)
         make_identity(nc, ident[:])
+        ident_bf = consts.tile([P, P], BF16)
+        make_identity(nc, ident_bf[:])
+        twice_ident = consts.tile([P, P], BF16)
+        nc.vector.tensor_single_scalar(out=twice_ident[:], in_=ident_bf[:], scalar=2.0, op=ALU.mult)
+        minus_ident = consts.tile([P, P], BF16)
+        nc.vector.tensor_single_scalar(out=minus_ident[:], in_=ident_bf[:], scalar=-1.0, op=ALU.mult)
         one_col = consts.tile([P, 1], F32)
         nc.vector.memset(one_col[:], 1.0)
         eps_col = consts.tile([P, 1], F32)
@@ -96,7 +102,7 @@ def tile_kanlayer_pa_kernel(tc, x, base_weight, spline_weight, out):
             natural[r] = (x_nat, bw_nat, sw_nat)
 
         def transpose_row_tile(natural_words, grouped_words):
-            bank = psum.tile([P, WORD_BLOCKS, P], F32, tag="bank")
+            bank = psum.tile([P, WORD_BLOCKS, P], F32, bufs=4)
             for w in range(WORD_BLOCKS):
                 nc.tensor.transpose(bank[:, w, :], natural_words[:, w * P : (w + 1) * P], ident[:])
             nc.scalar.copy(
@@ -147,27 +153,31 @@ def tile_kanlayer_pa_kernel(tc, x, base_weight, spline_weight, out):
             abs_x[j] = a
 
         def clamp_at_one(j):
-            twice_min1 = work.tile([P, TILE_COLS], BF16)
-            nc.vector.tensor_scalar(
-                out=twice_min1[:], in0=abs_x[j][:], scalar1=1.0, scalar2=2.0, op0=ALU.min, op1=ALU.mult
-            )
-            clamped_one[j] = twice_min1
+            min1 = work.tile([P, TILE_COLS], BF16)
+            nc.vector.tensor_single_scalar(out=min1[:], in_=abs_x[j][:], scalar=1.0, op=ALU.min)
+            clamped_one[j] = min1
 
         def clamp_at_two(j):
-            min2 = work.tile([P, TILE_COLS], BF16, bufs=1)
+            min2 = work.tile([P, TILE_COLS], BF16)
             nc.vector.tensor_single_scalar(out=min2[:], in_=abs_x[j][:], scalar=2.0, op=ALU.min)
             clamped_two[j] = min2
 
         def make_side_hat(j):
-            side = work.tile([P, TILE_COLS], BF16)
-            nc.vector.tensor_tensor(out=side[:], in0=clamped_one[j][:], in1=clamped_two[j][:], op=ALU.subtract)
-            side_hat[j] = side
+            halves = []
+            for n in range(TILE_COLS // N_TILE):
+                cols = slice(n * N_TILE, (n + 1) * N_TILE)
+                side = psum.tile([P, N_TILE], F32)
+                nc.tensor.matmul(side[:], lhsT=twice_ident[:], rhs=clamped_one[j][:, cols], start=True, stop=False)
+                nc.tensor.matmul(side[:], lhsT=minus_ident[:], rhs=clamped_two[j][:, cols], start=False, stop=True)
+                halves.append(side)
+            side_hat[j] = halves
 
         def square_hats(j):
             r_side = work.tile([P, TILE_COLS], F32, bufs=LOG_GROUP + 2)
-            nc.scalar.activation(out=r_side[:], in_=side_hat[j][:], func=ACT.Square)
+            for n, side in enumerate(side_hat[j]):
+                nc.scalar.activation(out=r_side[:, n * N_TILE : (n + 1) * N_TILE], in_=side[:], func=ACT.Square)
             r_centre = work.tile([P, TILE_COLS], F32, bufs=LOG_GROUP + 2)
-            nc.scalar.activation(out=r_centre[:], in_=clamped_one[j][:], func=ACT.Square, scale=-0.5, bias=one_col[:])
+            nc.scalar.activation(out=r_centre[:], in_=clamped_one[j][:], func=ACT.Square, scale=-1.0, bias=one_col[:])
             squares[j] = (r_side, r_centre)
 
         def add_squares(j):
@@ -236,7 +246,7 @@ def tile_kanlayer_pa_kernel(tc, x, base_weight, spline_weight, out):
             codes, scales = quantised[j]
             banks = []
             for n in range(N_TILES):
-                acc = psum.tile([P, N_TILE], F32, tag="bank")
+                acc = psum.tile([P, N_TILE], F32)
                 banks.append(acc)
             for k in range(PASSES):
                 rows = slice(k * P, (k + 1) * P)
@@ -281,6 +291,7 @@ def tile_kanlayer_pa_kernel(tc, x, base_weight, spline_weight, out):
                 if in_range(summed) and summed % LOG_GROUP == LOG_GROUP - 1:
                     for member in range(summed - LOG_GROUP + 1, summed + 1):
                         take_exp(member)
+                run(store, done - 1)
                 run(clamp_at_one, begun)
                 run(scale_side, done)
                 run(clamp_at_two, begun)
@@ -293,4 +304,3 @@ def tile_kanlayer_pa_kernel(tc, x, base_weight, spline_weight, out):
                 run(quantise_right, done)
                 run(quantise_left, done)
                 run(multiply, done)
-                run(store, done - 1)

@@ -38,7 +38,8 @@ FLOPS = 2 * ROWS * ROWS * FEATURES * MATRICES
 
 CLEAR_SIGNS = 0x7FFF7FFF
 
-LOAD_AHEAD = 2
+SPLINE_AHEAD = 2
+LOAD_AHEAD = 1
 WEIGHT_LAG = 2
 BASIS_SHIFT = ROW_TILES - 1 + WEIGHT_LAG
 STEPS = BASIS_SHIFT + ROW_TILES + 1
@@ -50,23 +51,19 @@ def tile_kanlayer_pa_kernel(tc, x, base_weight, spline_weight, out):
     with ExitStack() as ctx:
         consts = ctx.enter_context(tc.tile_pool(name="consts", bufs=1))
         keep = ctx.enter_context(tc.tile_pool(name="keep", bufs=1))
-        loads = ctx.enter_context(tc.tile_pool(name="loads", bufs=LOAD_AHEAD + 1))
+        loads = ctx.enter_context(tc.tile_pool(name="loads", bufs=SPLINE_AHEAD + 1))
         prep = ctx.enter_context(tc.tile_pool(name="prep", bufs=2))
         work = ctx.enter_context(tc.tile_pool(name="work", bufs=2))
-        psum = ctx.enter_context(tc.psum_pool(name="psum", bufs=2))
+        psum = ctx.enter_context(tc.psum_pool(name="psum", bufs=8))
 
         ident = consts.tile([P, P], F32)
         make_identity(nc, ident[:])
-        ident_bf = consts.tile([P, P], BF16)
-        make_identity(nc, ident_bf[:])
-        twice_ident = consts.tile([P, P], BF16)
-        nc.vector.tensor_single_scalar(out=twice_ident[:], in_=ident_bf[:], scalar=2.0, op=ALU.mult)
-        minus_ident = consts.tile([P, P], BF16)
-        nc.vector.tensor_single_scalar(out=minus_ident[:], in_=ident_bf[:], scalar=-1.0, op=ALU.mult)
         one_col = consts.tile([P, 1], F32)
         nc.vector.memset(one_col[:], 1.0)
         eps_col = consts.tile([P, 1], F32)
         nc.vector.memset(eps_col[:], BASIS_EPS)
+        first_log = consts.tile([P, 1], F32)
+        nc.scalar.activation(out=first_log[:], in_=one_col[:], func=ACT.Ln)
 
         x_grouped = keep.tile([P, ROW_TILES * TILE_COLS], BF16, align_bytes=64)
         x_grouped_words = x_grouped[:].bitcast(F32)
@@ -75,6 +72,7 @@ def tile_kanlayer_pa_kernel(tc, x, base_weight, spline_weight, out):
         w_scales = keep.tile([P, PASSES, ROWS], U8, align_bytes=64)
 
         natural = {}
+        natural_spline = {}
         grouped_weights = {}
         abs_x = {}
         clamped_one = {}
@@ -91,18 +89,22 @@ def tile_kanlayer_pa_kernel(tc, x, base_weight, spline_weight, out):
         def in_range(j):
             return 0 <= j < ROW_TILES
 
-        def load_row_tile(r):
+        def load_spline_tile(r):
             rows = slice(r * P, (r + 1) * P)
             sw_nat = loads.tile([P, FEATURES * GRID], BF16)
             nc.sync.dma_start(out=sw_nat[:], in_=spline_weight[rows, :, :].rearrange("o i g -> o (i g)"))
+            natural_spline[r] = sw_nat
+
+        def load_row_tile(r):
+            rows = slice(r * P, (r + 1) * P)
             x_nat = loads.tile([P, FEATURES], BF16)
             nc.sync.dma_start(out=x_nat[:], in_=x[rows, :])
             bw_nat = loads.tile([P, FEATURES], BF16)
             nc.sync.dma_start(out=bw_nat[:], in_=base_weight[rows, :])
-            natural[r] = (x_nat, bw_nat, sw_nat)
+            natural[r] = (x_nat, bw_nat)
 
         def transpose_row_tile(natural_words, grouped_words):
-            bank = psum.tile([P, WORD_BLOCKS, P], F32, bufs=4)
+            bank = psum.tile([P, WORD_BLOCKS, P], F32, tag="bank")
             for w in range(WORD_BLOCKS):
                 nc.tensor.transpose(bank[:, w, :], natural_words[:, w * P : (w + 1) * P], ident[:])
             nc.scalar.copy(
@@ -111,7 +113,8 @@ def tile_kanlayer_pa_kernel(tc, x, base_weight, spline_weight, out):
             )
 
         def prepare_row_tile(r):
-            x_nat, bw_nat, sw_nat = natural[r]
+            x_nat, bw_nat = natural[r]
+            sw_nat = natural_spline[r]
             words = TILE_COLS // 2
             w_grouped = prep.tile([P, MATRICES * TILE_COLS], BF16, bufs=WEIGHT_LAG + 1, align_bytes=64)
             w_grouped_words = w_grouped[:].bitcast(F32)
@@ -153,31 +156,27 @@ def tile_kanlayer_pa_kernel(tc, x, base_weight, spline_weight, out):
             abs_x[j] = a
 
         def clamp_at_one(j):
-            min1 = work.tile([P, TILE_COLS], BF16)
-            nc.vector.tensor_single_scalar(out=min1[:], in_=abs_x[j][:], scalar=1.0, op=ALU.min)
-            clamped_one[j] = min1
+            twice_min1 = work.tile([P, TILE_COLS], BF16)
+            nc.vector.tensor_scalar(
+                out=twice_min1[:], in0=abs_x[j][:], scalar1=1.0, scalar2=2.0, op0=ALU.min, op1=ALU.mult
+            )
+            clamped_one[j] = twice_min1
 
         def clamp_at_two(j):
-            min2 = work.tile([P, TILE_COLS], BF16)
+            min2 = work.tile([P, TILE_COLS], BF16, bufs=1)
             nc.vector.tensor_single_scalar(out=min2[:], in_=abs_x[j][:], scalar=2.0, op=ALU.min)
             clamped_two[j] = min2
 
         def make_side_hat(j):
-            halves = []
-            for n in range(TILE_COLS // N_TILE):
-                cols = slice(n * N_TILE, (n + 1) * N_TILE)
-                side = psum.tile([P, N_TILE], F32)
-                nc.tensor.matmul(side[:], lhsT=twice_ident[:], rhs=clamped_one[j][:, cols], start=True, stop=False)
-                nc.tensor.matmul(side[:], lhsT=minus_ident[:], rhs=clamped_two[j][:, cols], start=False, stop=True)
-                halves.append(side)
-            side_hat[j] = halves
+            side = work.tile([P, TILE_COLS], BF16)
+            nc.vector.tensor_tensor(out=side[:], in0=clamped_one[j][:], in1=clamped_two[j][:], op=ALU.subtract)
+            side_hat[j] = side
 
         def square_hats(j):
             r_side = work.tile([P, TILE_COLS], F32, bufs=LOG_GROUP + 2)
-            for n, side in enumerate(side_hat[j]):
-                nc.scalar.activation(out=r_side[:, n * N_TILE : (n + 1) * N_TILE], in_=side[:], func=ACT.Square)
+            nc.scalar.activation(out=r_side[:], in_=side_hat[j][:], func=ACT.Square)
             r_centre = work.tile([P, TILE_COLS], F32, bufs=LOG_GROUP + 2)
-            nc.scalar.activation(out=r_centre[:], in_=clamped_one[j][:], func=ACT.Square, scale=-1.0, bias=one_col[:])
+            nc.scalar.activation(out=r_centre[:], in_=clamped_one[j][:], func=ACT.Square, scale=-0.5, bias=one_col[:])
             squares[j] = (r_side, r_centre)
 
         def add_squares(j):
@@ -246,7 +245,7 @@ def tile_kanlayer_pa_kernel(tc, x, base_weight, spline_weight, out):
             codes, scales = quantised[j]
             banks = []
             for n in range(N_TILES):
-                acc = psum.tile([P, N_TILE], F32)
+                acc = psum.tile([P, N_TILE], F32, tag="bank")
                 banks.append(acc)
             for k in range(PASSES):
                 rows = slice(k * P, (k + 1) * P)
@@ -274,15 +273,19 @@ def tile_kanlayer_pa_kernel(tc, x, base_weight, spline_weight, out):
                 stage(j)
 
         with tc.manual_schedule():
+            for r in range(SPLINE_AHEAD):
+                load_spline_tile(r)
             for r in range(LOAD_AHEAD):
                 load_row_tile(r)
             for step in range(STEPS):
+                run(load_spline_tile, step + SPLINE_AHEAD)
                 run(load_row_tile, step + LOAD_AHEAD)
                 run(prepare_row_tile, step)
                 run(quantise_weights, step - WEIGHT_LAG)
                 done = step - BASIS_SHIFT
                 summed = done + LOG_GROUP
                 begun = summed + 2
+                run(quantise_x, done)
                 run(mark_positive, done)
                 run(take_abs, begun)
                 run(add_squares, summed)
@@ -291,16 +294,15 @@ def tile_kanlayer_pa_kernel(tc, x, base_weight, spline_weight, out):
                 if in_range(summed) and summed % LOG_GROUP == LOG_GROUP - 1:
                     for member in range(summed - LOG_GROUP + 1, summed + 1):
                         take_exp(member)
-                run(store, done - 1)
                 run(clamp_at_one, begun)
                 run(scale_side, done)
                 run(clamp_at_two, begun)
                 run(scale_centre, done)
                 run(make_side_hat, begun)
                 run(keep_right, done)
-                run(quantise_x, done)
-                run(keep_left, done)
                 run(quantise_centre, done)
+                run(keep_left, done)
                 run(quantise_right, done)
                 run(quantise_left, done)
                 run(multiply, done)
+                run(store, done - 1)

@@ -38,12 +38,11 @@ FLOPS = 2 * ROWS * ROWS * FEATURES * MATRICES
 
 CLEAR_SIGNS = 0x7FFF7FFF
 
-SPLINE_AHEAD = 2
-LOAD_AHEAD = 1
-WEIGHT_LAG = 2
-BASIS_SHIFT = ROW_TILES - 1 + WEIGHT_LAG
-STEPS = BASIS_SHIFT + ROW_TILES + 1
-LOG_GROUP = 4
+HALF = 4
+
+FIRST_BEAT = -3
+LAST_BEAT = ROW_TILES + 8
+CODE_TILES = 4
 
 
 def tile_kanlayer_pa_kernel(tc, x, base_weight, spline_weight, out):
@@ -51,13 +50,17 @@ def tile_kanlayer_pa_kernel(tc, x, base_weight, spline_weight, out):
     with ExitStack() as ctx:
         consts = ctx.enter_context(tc.tile_pool(name="consts", bufs=1))
         keep = ctx.enter_context(tc.tile_pool(name="keep", bufs=1))
-        loads = ctx.enter_context(tc.tile_pool(name="loads", bufs=SPLINE_AHEAD + 1))
-        prep = ctx.enter_context(tc.tile_pool(name="prep", bufs=2))
-        work = ctx.enter_context(tc.tile_pool(name="work", bufs=2))
+        loads = ctx.enter_context(tc.tile_pool(name="loads", bufs=3))
+        prep = ctx.enter_context(tc.tile_pool(name="prep", bufs=1))
+        work = ctx.enter_context(tc.tile_pool(name="work", bufs=1))
         psum = ctx.enter_context(tc.psum_pool(name="psum", bufs=8))
 
         ident = consts.tile([P, P], F32)
         make_identity(nc, ident[:])
+        plus_one = consts.tile([P, P], BF16)
+        nc.vector.tensor_copy(out=plus_one[:], in_=ident[:])
+        minus_one = consts.tile([P, P], BF16)
+        nc.vector.tensor_single_scalar(out=minus_one[:], in_=ident[:], scalar=-1.0, op=ALU.mult)
         one_col = consts.tile([P, 1], F32)
         nc.vector.memset(one_col[:], 1.0)
         eps_col = consts.tile([P, 1], F32)
@@ -71,65 +74,95 @@ def tile_kanlayer_pa_kernel(tc, x, base_weight, spline_weight, out):
         w_codes = keep.tile([P, PASSES, ROWS], U32, align_bytes=64)
         w_scales = keep.tile([P, PASSES, ROWS], U8, align_bytes=64)
 
-        natural = {}
+        natural_x = {}
+        natural_base = {}
         natural_spline = {}
+        sorted_spline = {}
         grouped_weights = {}
         abs_x = {}
         clamped_one = {}
         clamped_two = {}
         side_hat = {}
+        squares = {}
+        turned_sum = {}
+        normaliser = {}
+        turned_normaliser = {}
         is_positive = {}
         side_basis = {}
-        squares = {}
-        normaliser = {}
         basis = {}
         quantised = {}
         sums = {}
 
-        def in_range(j):
-            return 0 <= j < ROW_TILES
+        def load_x(j):
+            x_nat = loads.tile([P, FEATURES], BF16, bufs=ROW_TILES)
+            nc.sync.dma_start(out=x_nat[:], in_=x[j * P : (j + 1) * P, :])
+            natural_x[j] = x_nat
 
-        def load_spline_tile(r):
+        def load_weights(r):
             rows = slice(r * P, (r + 1) * P)
             sw_nat = loads.tile([P, FEATURES * GRID], BF16)
             nc.sync.dma_start(out=sw_nat[:], in_=spline_weight[rows, :, :].rearrange("o i g -> o (i g)"))
             natural_spline[r] = sw_nat
-
-        def load_row_tile(r):
-            rows = slice(r * P, (r + 1) * P)
-            x_nat = loads.tile([P, FEATURES], BF16)
-            nc.sync.dma_start(out=x_nat[:], in_=x[rows, :])
             bw_nat = loads.tile([P, FEATURES], BF16)
             nc.sync.dma_start(out=bw_nat[:], in_=base_weight[rows, :])
-            natural[r] = (x_nat, bw_nat)
+            natural_base[r] = bw_nat
 
-        def transpose_row_tile(natural_words, grouped_words):
+        def transpose_words(natural_words, grouped_words, copy):
             bank = psum.tile([P, WORD_BLOCKS, P], F32, tag="bank")
             for w in range(WORD_BLOCKS):
                 nc.tensor.transpose(bank[:, w, :], natural_words[:, w * P : (w + 1) * P], ident[:])
-            nc.scalar.copy(
+            copy(
                 out=grouped_words.rearrange("p (c r u) -> p c r u", c=MATRIX_PASSES, u=2),
                 in_=bank[:].rearrange("p (c u) r -> p c r u", u=2),
             )
 
-        def prepare_row_tile(r):
-            x_nat, bw_nat = natural[r]
-            sw_nat = natural_spline[r]
+        def prepare_x(j):
             words = TILE_COLS // 2
-            w_grouped = prep.tile([P, MATRICES * TILE_COLS], BF16, bufs=WEIGHT_LAG + 1, align_bytes=64)
-            w_grouped_words = w_grouped[:].bitcast(F32)
-            transpose_row_tile(x_nat[:].bitcast(F32), x_grouped_words[:, r * words : (r + 1) * words])
-            transpose_row_tile(bw_nat[:].bitcast(F32), w_grouped_words[:, 0:words])
+            copy = nc.scalar.copy if j < HALF else nc.vector.tensor_copy
+            transpose_words(natural_x[j][:].bitcast(F32), x_grouped_words[:, j * words : (j + 1) * words], copy)
+
+        def sort_spline(r):
             sorted_sw = prep.tile([P, GRID * FEATURES], BF16)
-            sorted_words = sorted_sw[:].bitcast(F32)
-            by_grid = sw_nat[:].rearrange("p (i g) -> p g i", g=GRID)
+            by_grid = natural_spline[r][:].rearrange("p (i g) -> p g i", g=GRID)
             for n, g in enumerate(GRID_ORDER):
                 nc.vector.tensor_copy(out=sorted_sw[:, n * FEATURES : (n + 1) * FEATURES], in_=by_grid[:, g, :])
-                transpose_row_tile(
-                    sorted_words[:, n * words : (n + 1) * words],
-                    w_grouped_words[:, (1 + n) * words : (2 + n) * words],
-                )
+            sorted_spline[r] = sorted_sw
+
+        def prepare_base(r):
+            w_grouped = prep.tile([P, MATRICES * TILE_COLS], BF16, bufs=2, align_bytes=64)
             grouped_weights[r] = w_grouped
+            words = TILE_COLS // 2
+            transpose_words(
+                natural_base[r][:].bitcast(F32), w_grouped[:].bitcast(F32)[:, 0:words], nc.vector.tensor_copy
+            )
+
+        def prepare_spline(r, n):
+            w_grouped = grouped_weights[r]
+            if r < HALF:
+                words = TILE_COLS // 2
+                transpose_words(
+                    sorted_spline[r][:].bitcast(F32)[:, n * words : (n + 1) * words],
+                    w_grouped[:].bitcast(F32)[:, (1 + n) * words : (2 + n) * words],
+                    nc.scalar.copy,
+                )
+                return
+            bank = psum.tile([P, MATRIX_PASSES * PACK, P], BF16, tag="bank")
+            step = 2 * GRID
+            for c in range(MATRIX_PASSES):
+                for t in range(PACK):
+                    feature = c * P * PACK + (t // 2) * 2 * P + t % 2
+                    first = GRID * feature + GRID_ORDER[n]
+                    nc.tensor.transpose(
+                        bank[:, c * PACK + t, :],
+                        natural_spline[r][:, first : first + step * (P - 1) + 1 : step],
+                        plus_one[:],
+                    )
+            nc.scalar.copy(
+                out=w_grouped[:, (1 + n) * TILE_COLS : (2 + n) * TILE_COLS].rearrange(
+                    "p (c r t) -> p c r t", c=MATRIX_PASSES, t=PACK
+                ),
+                in_=bank[:].rearrange("p (c t) r -> p c r t", t=PACK),
+            )
 
         def quantise_weights(r):
             w_grouped = grouped_weights[r]
@@ -144,9 +177,12 @@ def tile_kanlayer_pa_kernel(tc, x, base_weight, spline_weight, out):
         def x_tile(j):
             return x_grouped[:, j * TILE_COLS : (j + 1) * TILE_COLS]
 
+        def pass_cols(c):
+            return slice(c * PASS_COLS, (c + 1) * PASS_COLS)
+
         def take_abs(j):
             words = TILE_COLS // 2
-            a = work.tile([P, TILE_COLS], BF16, bufs=1)
+            a = work.tile([P, TILE_COLS], BF16)
             nc.vector.tensor_single_scalar(
                 out=a[:].bitcast(I32),
                 in_=x_grouped_bits[:, j * words : (j + 1) * words],
@@ -156,60 +192,115 @@ def tile_kanlayer_pa_kernel(tc, x, base_weight, spline_weight, out):
             abs_x[j] = a
 
         def clamp_at_one(j):
-            twice_min1 = work.tile([P, TILE_COLS], BF16)
+            twice_min1 = work.tile([P, TILE_COLS], BF16, bufs=5)
             nc.vector.tensor_scalar(
                 out=twice_min1[:], in0=abs_x[j][:], scalar1=1.0, scalar2=2.0, op0=ALU.min, op1=ALU.mult
             )
             clamped_one[j] = twice_min1
 
         def clamp_at_two(j):
-            min2 = work.tile([P, TILE_COLS], BF16, bufs=1)
+            min2 = work.tile([P, TILE_COLS], BF16, bufs=5)
             nc.vector.tensor_single_scalar(out=min2[:], in_=abs_x[j][:], scalar=2.0, op=ALU.min)
             clamped_two[j] = min2
 
         def make_side_hat(j):
-            side = work.tile([P, TILE_COLS], BF16)
-            nc.vector.tensor_tensor(out=side[:], in0=clamped_one[j][:], in1=clamped_two[j][:], op=ALU.subtract)
-            side_hat[j] = side
+            halves = []
+            for c in range(MATRIX_PASSES):
+                side = psum.tile([P, PASS_COLS], F32, tag="bank")
+                nc.tensor.matmul(
+                    side[:], lhsT=plus_one[:], rhs=clamped_one[j][:, pass_cols(c)], start=True, stop=False
+                )
+                nc.tensor.matmul(
+                    side[:], lhsT=minus_one[:], rhs=clamped_two[j][:, pass_cols(c)], start=False, stop=True
+                )
+                halves.append(side)
+            side_hat[j] = halves
 
         def square_hats(j):
-            r_side = work.tile([P, TILE_COLS], F32, bufs=LOG_GROUP + 2)
-            nc.scalar.activation(out=r_side[:], in_=side_hat[j][:], func=ACT.Square)
-            r_centre = work.tile([P, TILE_COLS], F32, bufs=LOG_GROUP + 2)
+            r_side = work.tile([P, TILE_COLS], F32, bufs=5)
+            for c in range(MATRIX_PASSES):
+                nc.scalar.activation(out=r_side[:, pass_cols(c)], in_=side_hat[j][c][:], func=ACT.Square)
+            r_centre = work.tile([P, TILE_COLS], F32, bufs=5)
             nc.scalar.activation(out=r_centre[:], in_=clamped_one[j][:], func=ACT.Square, scale=-0.5, bias=one_col[:])
             squares[j] = (r_side, r_centre)
 
-        def add_squares(j):
+        def turned_on_tensor(j):
+            return j < HALF
+
+        def turn_and_add_squares(j):
             r_side, r_centre = squares[j]
-            norm = work.tile([P, TILE_COLS], F32, bufs=LOG_GROUP + 1)
-            nc.vector.tensor_tensor(out=norm[:], in0=r_side[:], in1=r_centre[:], op=ALU.add)
+            halves = []
+            for c in range(MATRIX_PASSES):
+                bank = psum.tile([P, PASS_COLS], F32, tag="bank")
+                for b in range(PASS_COLS // P):
+                    block = bank[:, b * P : (b + 1) * P]
+                    cols = slice(c * PASS_COLS + b * P, c * PASS_COLS + (b + 1) * P)
+                    nc.tensor.matmul(
+                        block, lhsT=r_side[:, cols], rhs=ident[:], is_transpose=True, start=True, stop=False
+                    )
+                    nc.tensor.matmul(
+                        block, lhsT=r_centre[:, cols], rhs=ident[:], is_transpose=True, start=False, stop=True
+                    )
+                halves.append(bank)
+            turned_sum[j] = halves
+
+        def add_squares(j):
+            norm = work.tile([P, TILE_COLS], F32, tag="norm", bufs=4)
+            nc.vector.tensor_tensor(out=norm[:], in0=squares[j][0][:], in1=squares[j][1][:], op=ALU.add)
             normaliser[j] = norm
 
         def take_log(j):
-            norm = normaliser[j]
-            nc.scalar.activation(out=norm[:], in_=norm[:], func=ACT.Ln, bias=eps_col[:])
+            if not turned_on_tensor(j):
+                norm = normaliser[j]
+                nc.scalar.activation(out=norm[:], in_=norm[:], func=ACT.Ln, bias=eps_col[:])
+                return
+            norm = work.tile([P, TILE_COLS], F32, tag="norm", bufs=4)
+            for c in range(MATRIX_PASSES):
+                nc.scalar.activation(
+                    out=norm[:, pass_cols(c)], in_=turned_sum[j][c][:], func=ACT.Ln, bias=eps_col[:]
+                )
+            normaliser[j] = norm
 
         def take_exp(j):
             norm = normaliser[j]
             nc.scalar.activation(out=norm[:], in_=norm[:], func=ACT.Exp, scale=-1.0)
 
+        def turn_back(j):
+            halves = []
+            for c in range(MATRIX_PASSES):
+                bank = psum.tile([P, PASS_COLS], F32, tag="bank")
+                for b in range(PASS_COLS // P):
+                    cols = slice(c * PASS_COLS + b * P, c * PASS_COLS + (b + 1) * P)
+                    nc.tensor.transpose(bank[:, b * P : (b + 1) * P], normaliser[j][:, cols], ident[:])
+                halves.append(bank)
+            turned_normaliser[j] = halves
+
         def mark_positive(j):
-            positive = work.tile([P, TILE_COLS], BF16, bufs=1)
+            positive = work.tile([P, TILE_COLS], BF16)
             nc.vector.tensor_single_scalar(out=positive[:], in_=x_tile(j), scalar=0.0, op=ALU.is_gt)
             is_positive[j] = positive
 
+        def scale_squares(out, square, j):
+            if not turned_on_tensor(j):
+                nc.vector.tensor_tensor(out=out, in0=square[:], in1=normaliser[j][:], op=ALU.mult)
+                return
+            for c in range(MATRIX_PASSES):
+                nc.vector.tensor_tensor(
+                    out=out[:, pass_cols(c)], in0=square[:, pass_cols(c)], in1=turned_normaliser[j][c][:], op=ALU.mult
+                )
+
         def scale_side(j):
-            b_side = work.tile([P, TILE_COLS], BF16, bufs=1)
-            nc.vector.tensor_tensor(out=b_side[:], in0=squares[j][0][:], in1=normaliser[j][:], op=ALU.mult)
+            b_side = work.tile([P, TILE_COLS], BF16)
+            scale_squares(b_side[:], squares[j][0], j)
             side_basis[j] = b_side
 
         def plane(j, n):
             return basis[j][:, n * TILE_COLS : (n + 1) * TILE_COLS]
 
         def scale_centre(j):
-            planes = work.tile([P, GRID * TILE_COLS], BF16, bufs=1, align_bytes=64)
+            planes = work.tile([P, GRID * TILE_COLS], BF16, align_bytes=64)
             basis[j] = planes
-            nc.vector.tensor_tensor(out=plane(j, CENTRE), in0=squares[j][1][:], in1=normaliser[j][:], op=ALU.mult)
+            scale_squares(plane(j, CENTRE), squares[j][1], j)
 
         def keep_right(j):
             nc.vector.tensor_tensor(out=plane(j, RIGHT), in0=side_basis[j][:], in1=is_positive[j][:], op=ALU.mult)
@@ -227,32 +318,25 @@ def tile_kanlayer_pa_kernel(tc, x, base_weight, spline_weight, out):
             )
 
         def quantise_x(j):
-            codes = work.tile([P, PASSES * P], U32, align_bytes=64)
-            scales = work.tile([P, PASSES * P], U8, align_bytes=64)
+            codes = work.tile([P, PASSES * P], U32, bufs=CODE_TILES, align_bytes=64)
+            scales = work.tile([P, PASSES * P], U8, bufs=CODE_TILES, align_bytes=64)
             quantised[j] = (codes, scales)
             quantise_matrix(j, 0, x_tile(j))
 
-        def quantise_centre(j):
-            quantise_matrix(j, 1 + CENTRE, plane(j, CENTRE))
+        def quantise_plane(j, n):
+            quantise_matrix(j, 1 + n, plane(j, n))
 
-        def quantise_right(j):
-            quantise_matrix(j, 1 + RIGHT, plane(j, RIGHT))
-
-        def quantise_left(j):
-            quantise_matrix(j, 1 + LEFT, plane(j, LEFT))
-
-        def multiply(j):
+        def multiply(j, tiles):
             codes, scales = quantised[j]
-            banks = []
-            for n in range(N_TILES):
+            for n in tiles:
                 acc = psum.tile([P, N_TILE], F32, tag="bank")
-                banks.append(acc)
+                sums[j, n] = acc
             for k in range(PASSES):
                 rows = slice(k * P, (k + 1) * P)
-                for n in range(N_TILES):
+                for n in tiles:
                     cols = slice(n * N_TILE, (n + 1) * N_TILE)
                     nc.tensor.matmul_mx(
-                        out=banks[n][:],
+                        out=sums[j, n][:],
                         lhsT=codes[:, rows].bitcast(FP8X4),
                         lhsT_scale=scales[:, rows],
                         rhs=w_codes[:, k, cols].bitcast(FP8X4),
@@ -260,49 +344,63 @@ def tile_kanlayer_pa_kernel(tc, x, base_weight, spline_weight, out):
                         start=(k == 0),
                         stop=(k == PASSES - 1),
                     )
-            sums[j] = banks
 
-        def store(j):
-            for n, acc in enumerate(sums[j]):
-                result = work.tile([P, N_TILE], F32, bufs=3)
-                nc.scalar.copy(out=result[:], in_=acc[:])
-                nc.sync.dma_start(out=out[j * P : (j + 1) * P, n * N_TILE : (n + 1) * N_TILE], in_=result[:])
+        def store(j, n):
+            result = work.tile([P, N_TILE], F32, bufs=3)
+            nc.scalar.copy(out=result[:], in_=sums[j, n][:])
+            nc.sync.dma_start(out=out[j * P : (j + 1) * P, n * N_TILE : (n + 1) * N_TILE], in_=result[:])
 
-        def run(stage, j):
-            if in_range(j):
-                stage(j)
+        def run(stage, beat, first=None, second=None, args=()):
+            for half, offset in ((range(HALF), first), (range(HALF, ROW_TILES), second)):
+                if offset is not None and beat - offset in half:
+                    stage(beat - offset, *args)
 
         with tc.manual_schedule():
-            for r in range(SPLINE_AHEAD):
-                load_spline_tile(r)
-            for r in range(LOAD_AHEAD):
-                load_row_tile(r)
-            for step in range(STEPS):
-                run(load_spline_tile, step + SPLINE_AHEAD)
-                run(load_row_tile, step + LOAD_AHEAD)
-                run(prepare_row_tile, step)
-                run(quantise_weights, step - WEIGHT_LAG)
-                done = step - BASIS_SHIFT
-                summed = done + LOG_GROUP
-                begun = summed + 2
-                run(quantise_x, done)
-                run(mark_positive, done)
-                run(take_abs, begun)
-                run(add_squares, summed)
-                run(square_hats, summed + 1)
-                run(take_log, summed)
-                if in_range(summed) and summed % LOG_GROUP == LOG_GROUP - 1:
-                    for member in range(summed - LOG_GROUP + 1, summed + 1):
-                        take_exp(member)
-                run(clamp_at_one, begun)
-                run(scale_side, done)
-                run(clamp_at_two, begun)
-                run(scale_centre, done)
-                run(make_side_hat, begun)
-                run(keep_right, done)
-                run(quantise_centre, done)
-                run(keep_left, done)
-                run(quantise_right, done)
-                run(quantise_left, done)
-                run(multiply, done)
-                run(store, done - 1)
+            for j in range(HALF):
+                load_x(j)
+            for beat in range(FIRST_BEAT, LAST_BEAT):
+                run(load_weights, beat, -1, -1)
+                run(load_x, beat, None, -6)
+                run(make_side_hat, beat, -1, 0)
+                run(square_hats, beat, -1, 1)
+                run(mark_positive, beat, 5, 6)
+                run(turn_and_add_squares, beat, 1, None)
+                run(take_log, beat, 1, 2)
+                run(sort_spline, beat, 1, None)
+                if beat < FIRST_BEAT + HALF // 2:
+                    for j in (2 * (beat - FIRST_BEAT), 2 * (beat - FIRST_BEAT) + 1):
+                        prepare_x(j)
+                run(prepare_x, beat, None, -5)
+                run(quantise_x, beat, 5, 6)
+                run(scale_side, beat, 5, 6)
+                run(take_abs, beat, -3, -3)
+                run(scale_centre, beat, 5, 6)
+                run(clamp_at_one, beat, -3, -3)
+                if beat in (HALF, ROW_TILES + 1):
+                    group = range(HALF) if beat == HALF else range(HALF, ROW_TILES)
+                    for j in group:
+                        take_exp(j)
+                run(keep_right, beat, 5, 6)
+                run(quantise_weights, beat, 2, 2)
+                run(quantise_plane, beat, 5, 6, (CENTRE,))
+                run(keep_left, beat, 5, 6)
+                run(quantise_plane, beat, 5, 6, (RIGHT,))
+                run(prepare_base, beat, 1, 1)
+                run(prepare_spline, beat, 1, 1, (0,))
+                run(add_squares, beat, None, 1)
+                run(quantise_plane, beat, 5, 6, (LEFT,))
+                run(prepare_spline, beat, 1, 1, (1,))
+                run(clamp_at_two, beat, -3, -3)
+                run(prepare_spline, beat, 1, 1, (2,))
+                run(turn_back, beat, 4, None)
+                run(store, beat, 7, None, (0,))
+                if beat == ROW_TILES + 3:
+                    for j in range(HALF):
+                        store(j, 1)
+                for n in range(N_TILES):
+                    run(store, beat, None, 8, (n,))
+                run(multiply, beat, 6, None, ((0,),))
+                if beat == ROW_TILES + 2:
+                    for j in range(HALF):
+                        multiply(j, (1,))
+                run(multiply, beat, None, 7, (range(N_TILES),))

@@ -118,7 +118,7 @@ def tile_kanlayer_pa_kernel(tc, x, base_weight, spline_weight, out):
 
         def prepare_x(j):
             words = TILE_COLS // 2
-            copy = nc.scalar.copy if j < HALF else nc.vector.tensor_copy
+            copy = nc.scalar.copy
             transpose_words(natural_x[j][:].bitcast(F32), x_grouped_words[:, j * words : (j + 1) * words], copy)
 
         def sort_spline(r):
@@ -133,35 +133,18 @@ def tile_kanlayer_pa_kernel(tc, x, base_weight, spline_weight, out):
             grouped_weights[r] = w_grouped
             words = TILE_COLS // 2
             transpose_words(
-                natural_base[r][:].bitcast(F32), w_grouped[:].bitcast(F32)[:, 0:words], nc.vector.tensor_copy
+                natural_base[r][:].bitcast(F32),
+                w_grouped[:].bitcast(F32)[:, 0:words],
+                nc.vector.tensor_copy if r < HALF else nc.scalar.copy,
             )
 
         def prepare_spline(r, n):
             w_grouped = grouped_weights[r]
-            if r < HALF:
-                words = TILE_COLS // 2
-                transpose_words(
-                    sorted_spline[r][:].bitcast(F32)[:, n * words : (n + 1) * words],
-                    w_grouped[:].bitcast(F32)[:, (1 + n) * words : (2 + n) * words],
-                    nc.scalar.copy,
-                )
-                return
-            bank = psum.tile([P, MATRIX_PASSES * PACK, P], BF16, tag="bank")
-            step = 2 * GRID
-            for c in range(MATRIX_PASSES):
-                for t in range(PACK):
-                    feature = c * P * PACK + (t // 2) * 2 * P + t % 2
-                    first = GRID * feature + GRID_ORDER[n]
-                    nc.tensor.transpose(
-                        bank[:, c * PACK + t, :],
-                        natural_spline[r][:, first : first + step * (P - 1) + 1 : step],
-                        plus_one[:],
-                    )
-            nc.scalar.copy(
-                out=w_grouped[:, (1 + n) * TILE_COLS : (2 + n) * TILE_COLS].rearrange(
-                    "p (c r t) -> p c r t", c=MATRIX_PASSES, t=PACK
-                ),
-                in_=bank[:].rearrange("p (c t) r -> p c r t", t=PACK),
+            words = TILE_COLS // 2
+            transpose_words(
+                sorted_spline[r][:].bitcast(F32)[:, n * words : (n + 1) * words],
+                w_grouped[:].bitcast(F32)[:, (1 + n) * words : (2 + n) * words],
+                nc.scalar.copy,
             )
 
         def quantise_weights(r):
@@ -366,7 +349,7 @@ def tile_kanlayer_pa_kernel(tc, x, base_weight, spline_weight, out):
                 run(mark_positive, beat, 5, 6)
                 run(turn_and_add_squares, beat, 1, None)
                 run(take_log, beat, 1, 2)
-                run(sort_spline, beat, 1, None)
+                run(sort_spline, beat, 1, 1)
                 if beat < FIRST_BEAT + HALF // 2:
                     for j in (2 * (beat - FIRST_BEAT), 2 * (beat - FIRST_BEAT) + 1):
                         prepare_x(j)

@@ -40,9 +40,11 @@ CLEAR_SIGNS = 0x7FFF7FFF
 
 HALF = 4
 
+TENSOR_SUMS = (0, 1, 6, 7)
+CODE_TILES = 2
 FIRST_BEAT = -3
-LAST_BEAT = ROW_TILES + 8
-CODE_TILES = 4
+LAST_BEAT = 20
+EXP_BEATS = (7, 13)
 
 
 def tile_kanlayer_pa_kernel(tc, x, base_weight, spline_weight, out):
@@ -94,15 +96,18 @@ def tile_kanlayer_pa_kernel(tc, x, base_weight, spline_weight, out):
         sums = {}
 
         def load_x(j):
-            x_nat = loads.tile([P, FEATURES], BF16, bufs=ROW_TILES)
+            x_nat = loads.tile([P, FEATURES], BF16)
             nc.sync.dma_start(out=x_nat[:], in_=x[j * P : (j + 1) * P, :])
             natural_x[j] = x_nat
 
-        def load_weights(r):
+        def load_spline(r):
             rows = slice(r * P, (r + 1) * P)
             sw_nat = loads.tile([P, FEATURES * GRID], BF16)
             nc.sync.dma_start(out=sw_nat[:], in_=spline_weight[rows, :, :].rearrange("o i g -> o (i g)"))
             natural_spline[r] = sw_nat
+
+        def load_base(r):
+            rows = slice(r * P, (r + 1) * P)
             bw_nat = loads.tile([P, FEATURES], BF16)
             nc.sync.dma_start(out=bw_nat[:], in_=base_weight[rows, :])
             natural_base[r] = bw_nat
@@ -118,11 +123,12 @@ def tile_kanlayer_pa_kernel(tc, x, base_weight, spline_weight, out):
 
         def prepare_x(j):
             words = TILE_COLS // 2
-            copy = nc.scalar.copy
-            transpose_words(natural_x[j][:].bitcast(F32), x_grouped_words[:, j * words : (j + 1) * words], copy)
+            transpose_words(
+                natural_x[j][:].bitcast(F32), x_grouped_words[:, j * words : (j + 1) * words], nc.scalar.copy
+            )
 
         def sort_spline(r):
-            sorted_sw = prep.tile([P, GRID * FEATURES], BF16)
+            sorted_sw = prep.tile([P, GRID * FEATURES], BF16, bufs=2)
             by_grid = natural_spline[r][:].rearrange("p (i g) -> p g i", g=GRID)
             for n, g in enumerate(GRID_ORDER):
                 nc.vector.tensor_copy(out=sorted_sw[:, n * FEATURES : (n + 1) * FEATURES], in_=by_grid[:, g, :])
@@ -133,9 +139,7 @@ def tile_kanlayer_pa_kernel(tc, x, base_weight, spline_weight, out):
             grouped_weights[r] = w_grouped
             words = TILE_COLS // 2
             transpose_words(
-                natural_base[r][:].bitcast(F32),
-                w_grouped[:].bitcast(F32)[:, 0:words],
-                nc.vector.tensor_copy if r < HALF else nc.scalar.copy,
+                natural_base[r][:].bitcast(F32), w_grouped[:].bitcast(F32)[:, 0:words], nc.vector.tensor_copy
             )
 
         def prepare_spline(r, n):
@@ -200,17 +204,19 @@ def tile_kanlayer_pa_kernel(tc, x, base_weight, spline_weight, out):
             side_hat[j] = halves
 
         def square_hats(j):
-            r_side = work.tile([P, TILE_COLS], F32, bufs=5)
+            r_side = work.tile([P, TILE_COLS], F32, bufs=6)
             for c in range(MATRIX_PASSES):
                 nc.scalar.activation(out=r_side[:, pass_cols(c)], in_=side_hat[j][c][:], func=ACT.Square)
-            r_centre = work.tile([P, TILE_COLS], F32, bufs=5)
+            r_centre = work.tile([P, TILE_COLS], F32, bufs=6)
             nc.scalar.activation(out=r_centre[:], in_=clamped_one[j][:], func=ACT.Square, scale=-0.5, bias=one_col[:])
             squares[j] = (r_side, r_centre)
 
         def turned_on_tensor(j):
-            return j < HALF
+            return j in TENSOR_SUMS
 
         def turn_and_add_squares(j):
+            if not turned_on_tensor(j):
+                return
             r_side, r_centre = squares[j]
             halves = []
             for c in range(MATRIX_PASSES):
@@ -228,7 +234,9 @@ def tile_kanlayer_pa_kernel(tc, x, base_weight, spline_weight, out):
             turned_sum[j] = halves
 
         def add_squares(j):
-            norm = work.tile([P, TILE_COLS], F32, tag="norm", bufs=4)
+            if turned_on_tensor(j):
+                return
+            norm = work.tile([P, TILE_COLS], F32, tag="norm", bufs=5)
             nc.vector.tensor_tensor(out=norm[:], in0=squares[j][0][:], in1=squares[j][1][:], op=ALU.add)
             normaliser[j] = norm
 
@@ -237,7 +245,7 @@ def tile_kanlayer_pa_kernel(tc, x, base_weight, spline_weight, out):
                 norm = normaliser[j]
                 nc.scalar.activation(out=norm[:], in_=norm[:], func=ACT.Ln, bias=eps_col[:])
                 return
-            norm = work.tile([P, TILE_COLS], F32, tag="norm", bufs=4)
+            norm = work.tile([P, TILE_COLS], F32, tag="norm", bufs=5)
             for c in range(MATRIX_PASSES):
                 nc.scalar.activation(
                     out=norm[:, pass_cols(c)], in_=turned_sum[j][c][:], func=ACT.Ln, bias=eps_col[:]
@@ -249,6 +257,8 @@ def tile_kanlayer_pa_kernel(tc, x, base_weight, spline_weight, out):
             nc.scalar.activation(out=norm[:], in_=norm[:], func=ACT.Exp, scale=-1.0)
 
         def turn_back(j):
+            if not turned_on_tensor(j):
+                return
             halves = []
             for c in range(MATRIX_PASSES):
                 bank = psum.tile([P, PASS_COLS], F32, tag="bank")
@@ -309,17 +319,18 @@ def tile_kanlayer_pa_kernel(tc, x, base_weight, spline_weight, out):
         def quantise_plane(j, n):
             quantise_matrix(j, 1 + n, plane(j, n))
 
-        def multiply(j, tiles):
+        def multiply(j):
             codes, scales = quantised[j]
-            for n in tiles:
+            banks = []
+            for n in range(N_TILES):
                 acc = psum.tile([P, N_TILE], F32, tag="bank")
-                sums[j, n] = acc
+                banks.append(acc)
             for k in range(PASSES):
                 rows = slice(k * P, (k + 1) * P)
-                for n in tiles:
+                for n in range(N_TILES):
                     cols = slice(n * N_TILE, (n + 1) * N_TILE)
                     nc.tensor.matmul_mx(
-                        out=sums[j, n][:],
+                        out=banks[n][:],
                         lhsT=codes[:, rows].bitcast(FP8X4),
                         lhsT_scale=scales[:, rows],
                         rhs=w_codes[:, k, cols].bitcast(FP8X4),
@@ -327,63 +338,54 @@ def tile_kanlayer_pa_kernel(tc, x, base_weight, spline_weight, out):
                         start=(k == 0),
                         stop=(k == PASSES - 1),
                     )
+            sums[j] = banks
 
-        def store(j, n):
-            result = work.tile([P, N_TILE], F32, bufs=3)
-            nc.scalar.copy(out=result[:], in_=sums[j, n][:])
-            nc.sync.dma_start(out=out[j * P : (j + 1) * P, n * N_TILE : (n + 1) * N_TILE], in_=result[:])
+        def store(j):
+            for n, acc in enumerate(sums[j]):
+                result = work.tile([P, N_TILE], F32, bufs=3)
+                nc.scalar.copy(out=result[:], in_=acc[:])
+                nc.sync.dma_start(out=out[j * P : (j + 1) * P, n * N_TILE : (n + 1) * N_TILE], in_=result[:])
 
-        def run(stage, beat, first=None, second=None, args=()):
+        def run(stage, beat, first, second, args=()):
             for half, offset in ((range(HALF), first), (range(HALF, ROW_TILES), second)):
                 if offset is not None and beat - offset in half:
                     stage(beat - offset, *args)
 
         with tc.manual_schedule():
-            for j in range(HALF):
-                load_x(j)
-            for beat in range(FIRST_BEAT, LAST_BEAT):
-                run(load_weights, beat, -1, -1)
-                run(load_x, beat, None, -6)
-                run(make_side_hat, beat, -1, 0)
-                run(square_hats, beat, -1, 1)
-                run(mark_positive, beat, 5, 6)
-                run(turn_and_add_squares, beat, 1, None)
-                run(take_log, beat, 1, 2)
-                run(sort_spline, beat, 1, 1)
-                if beat < FIRST_BEAT + HALF // 2:
-                    for j in (2 * (beat - FIRST_BEAT), 2 * (beat - FIRST_BEAT) + 1):
-                        prepare_x(j)
-                run(prepare_x, beat, None, -5)
-                run(quantise_x, beat, 5, 6)
-                run(scale_side, beat, 5, 6)
-                run(take_abs, beat, -3, -3)
-                run(scale_centre, beat, 5, 6)
-                run(clamp_at_one, beat, -3, -3)
-                if beat in (HALF, ROW_TILES + 1):
-                    group = range(HALF) if beat == HALF else range(HALF, ROW_TILES)
-                    for j in group:
-                        take_exp(j)
-                run(keep_right, beat, 5, 6)
-                run(quantise_weights, beat, 2, 2)
-                run(quantise_plane, beat, 5, 6, (CENTRE,))
-                run(keep_left, beat, 5, 6)
-                run(quantise_plane, beat, 5, 6, (RIGHT,))
-                run(prepare_base, beat, 1, 1)
-                run(prepare_spline, beat, 1, 1, (0,))
-                run(add_squares, beat, None, 1)
-                run(quantise_plane, beat, 5, 6, (LEFT,))
-                run(prepare_spline, beat, 1, 1, (1,))
-                run(clamp_at_two, beat, -3, -3)
-                run(prepare_spline, beat, 1, 1, (2,))
-                run(turn_back, beat, 4, None)
-                run(store, beat, 7, None, (0,))
-                if beat == ROW_TILES + 3:
-                    for j in range(HALF):
-                        store(j, 1)
-                for n in range(N_TILES):
-                    run(store, beat, None, 8, (n,))
-                run(multiply, beat, 6, None, ((0,),))
-                if beat == ROW_TILES + 2:
-                    for j in range(HALF):
-                        multiply(j, (1,))
-                run(multiply, beat, None, 7, (range(N_TILES),))
+            for beat in range(FIRST_BEAT, LAST_BEAT + 1):
+                run(load_x, beat, -1, None)
+                run(load_base, beat, -2, None)
+                run(load_spline, beat, -3, None)
+                run(load_x, beat, None, -3)
+                run(load_spline, beat, None, -2)
+                run(load_base, beat, None, -4)
+                for half in range(2):
+                    if beat == EXP_BEATS[half]:
+                        for j in range(half * HALF, (half + 1) * HALF):
+                            take_exp(j)
+                run(quantise_x, beat, 9, 11)
+                run(mark_positive, beat, 9, 11)
+                run(take_abs, beat, 0, 0)
+                run(clamp_at_one, beat, 0, 0)
+                run(scale_side, beat, 9, 11)
+                run(clamp_at_two, beat, 0, 0)
+                run(make_side_hat, beat, 1, 2)
+                run(scale_centre, beat, 9, 11)
+                run(square_hats, beat, 1, 2)
+                run(keep_right, beat, 9, 11)
+                run(quantise_plane, beat, 9, 11, (CENTRE,))
+                run(keep_left, beat, 9, 11)
+                run(turn_back, beat, 8, 9)
+                run(quantise_plane, beat, 9, 11, (RIGHT,))
+                run(sort_spline, beat, -2, -2)
+                run(prepare_base, beat, -1, -1)
+                for n in range(GRID):
+                    run(prepare_spline, beat, -1, -1, (n,))
+                run(take_log, beat, 3, 5)
+                run(quantise_plane, beat, 9, 11, (LEFT,))
+                run(quantise_weights, beat, 0, 0)
+                run(add_squares, beat, 2, 4)
+                run(multiply, beat, 10, 12)
+                run(store, beat, 11, 13)
+                run(turn_and_add_squares, beat, 2, 4)
+                run(prepare_x, beat, -1, -3)

@@ -42,6 +42,7 @@ HALF = 4
 
 TENSOR_SUMS = (0, 1, 6, 7)
 CODE_TILES = 2
+LAST_N_TILE = 256
 FIRST_BEAT = -3
 LAST_BEAT = 20
 EXP_BEATS = (7, 13)
@@ -319,32 +320,47 @@ def tile_kanlayer_pa_kernel(tc, x, base_weight, spline_weight, out):
         def quantise_plane(j, n):
             quantise_matrix(j, 1 + n, plane(j, n))
 
-        def multiply(j):
+        def add_passes(j, passes, n):
             codes, scales = quantised[j]
-            banks = []
-            for n in range(N_TILES):
-                acc = psum.tile([P, N_TILE], F32, tag="bank")
-                banks.append(acc)
-            for k in range(PASSES):
+            width = tile_width(j)
+            cols = slice(n * width, (n + 1) * width)
+            for k in passes:
                 rows = slice(k * P, (k + 1) * P)
-                for n in range(N_TILES):
-                    cols = slice(n * N_TILE, (n + 1) * N_TILE)
-                    nc.tensor.matmul_mx(
-                        out=banks[n][:],
-                        lhsT=codes[:, rows].bitcast(FP8X4),
-                        lhsT_scale=scales[:, rows],
-                        rhs=w_codes[:, k, cols].bitcast(FP8X4),
-                        rhs_scale=w_scales[:, k, cols],
-                        start=(k == 0),
-                        stop=(k == PASSES - 1),
-                    )
-            sums[j] = banks
+                nc.tensor.matmul_mx(
+                    out=sums[j][n][:, :width],
+                    lhsT=codes[:, rows].bitcast(FP8X4),
+                    lhsT_scale=scales[:, rows],
+                    rhs=w_codes[:, k, cols].bitcast(FP8X4),
+                    rhs_scale=w_scales[:, k, cols],
+                    start=(k == 0),
+                    stop=(k == PASSES - 1),
+                )
+
+        def tile_width(j):
+            return N_TILE if j < ROW_TILES - 1 else LAST_N_TILE
+
+        def multiply(j):
+            sums[j] = []
+            tiles = range(ROWS // tile_width(j))
+            for n in tiles:
+                acc = psum.tile([P, N_TILE], F32, tag="bank")
+                sums[j].append(acc)
+            early = PASSES if j < ROW_TILES - 1 else PASSES - MATRIX_PASSES
+            for k in range(early):
+                for n in tiles:
+                    add_passes(j, (k,), n)
+            for n in tiles:
+                add_passes(j, range(early, PASSES), n)
 
         def store(j):
+            width = tile_width(j)
             for n, acc in enumerate(sums[j]):
-                result = work.tile([P, N_TILE], F32, bufs=3)
-                nc.scalar.copy(out=result[:], in_=acc[:])
-                nc.sync.dma_start(out=out[j * P : (j + 1) * P, n * N_TILE : (n + 1) * N_TILE], in_=result[:])
+                result = work.tile([P, N_TILE], F32, bufs=4)
+                copy = nc.scalar.copy if j < ROW_TILES - 1 or n % 2 == 0 else nc.vector.tensor_copy
+                copy(out=result[:, :width], in_=acc[:, :width])
+                nc.sync.dma_start(
+                    out=out[j * P : (j + 1) * P, n * width : (n + 1) * width], in_=result[:, :width]
+                )
 
         def run(stage, beat, first, second, args=()):
             for half, offset in ((range(HALF), first), (range(HALF, ROW_TILES), second)):

@@ -40,11 +40,11 @@ CLEAR_SIGNS = 0x7FFF7FFF
 
 HALF = 4
 
-TENSOR_SUMS = (0, 1, 6, 7)
+TENSOR_SUMS = (0, 1, 2, 3)
 CODE_TILES = 2
 LAST_N_TILE = 256
-FIRST_BEAT = -3
-LAST_BEAT = 20
+FIRST_BEAT = -2
+LAST_BEAT = 19
 EXP_BEATS = (7, 13)
 
 
@@ -97,7 +97,7 @@ def tile_kanlayer_pa_kernel(tc, x, base_weight, spline_weight, out):
         sums = {}
 
         def load_x(j):
-            x_nat = loads.tile([P, FEATURES], BF16)
+            x_nat = loads.tile([P, FEATURES], BF16, bufs=2)
             nc.sync.dma_start(out=x_nat[:], in_=x[j * P : (j + 1) * P, :])
             natural_x[j] = x_nat
 
@@ -125,7 +125,9 @@ def tile_kanlayer_pa_kernel(tc, x, base_weight, spline_weight, out):
         def prepare_x(j):
             words = TILE_COLS // 2
             transpose_words(
-                natural_x[j][:].bitcast(F32), x_grouped_words[:, j * words : (j + 1) * words], nc.scalar.copy
+                natural_x[j][:].bitcast(F32),
+                x_grouped_words[:, j * words : (j + 1) * words],
+                nc.scalar.copy if j < HALF else nc.vector.tensor_copy,
             )
 
         def sort_spline(r):
@@ -140,7 +142,9 @@ def tile_kanlayer_pa_kernel(tc, x, base_weight, spline_weight, out):
             grouped_weights[r] = w_grouped
             words = TILE_COLS // 2
             transpose_words(
-                natural_base[r][:].bitcast(F32), w_grouped[:].bitcast(F32)[:, 0:words], nc.vector.tensor_copy
+                natural_base[r][:].bitcast(F32),
+                w_grouped[:].bitcast(F32)[:, 0:words],
+                nc.scalar.copy if r < HALF else nc.vector.tensor_copy,
             )
 
         def prepare_spline(r, n):
@@ -180,14 +184,14 @@ def tile_kanlayer_pa_kernel(tc, x, base_weight, spline_weight, out):
             abs_x[j] = a
 
         def clamp_at_one(j):
-            twice_min1 = work.tile([P, TILE_COLS], BF16, bufs=5)
+            twice_min1 = work.tile([P, TILE_COLS], BF16, bufs=3)
             nc.vector.tensor_scalar(
                 out=twice_min1[:], in0=abs_x[j][:], scalar1=1.0, scalar2=2.0, op0=ALU.min, op1=ALU.mult
             )
             clamped_one[j] = twice_min1
 
         def clamp_at_two(j):
-            min2 = work.tile([P, TILE_COLS], BF16, bufs=5)
+            min2 = work.tile([P, TILE_COLS], BF16, bufs=3)
             nc.vector.tensor_single_scalar(out=min2[:], in_=abs_x[j][:], scalar=2.0, op=ALU.min)
             clamped_two[j] = min2
 
@@ -369,39 +373,36 @@ def tile_kanlayer_pa_kernel(tc, x, base_weight, spline_weight, out):
 
         with tc.manual_schedule():
             for beat in range(FIRST_BEAT, LAST_BEAT + 1):
-                run(load_x, beat, -1, None)
-                run(load_base, beat, -2, None)
-                run(load_spline, beat, -3, None)
-                run(load_x, beat, None, -3)
-                run(load_spline, beat, None, -2)
-                run(load_base, beat, None, -4)
+                run(load_spline, beat, -2, -2)
+                run(load_x, beat, -2, -2)
+                run(load_base, beat, -2, -2)
+                run(prepare_x, beat, -1, 0)
+                run(take_log, beat, 4, 6)
                 for half in range(2):
                     if beat == EXP_BEATS[half]:
                         for j in range(half * HALF, (half + 1) * HALF):
                             take_exp(j)
-                run(quantise_x, beat, 9, 11)
-                run(mark_positive, beat, 9, 11)
-                run(take_abs, beat, 0, 0)
-                run(clamp_at_one, beat, 0, 0)
-                run(scale_side, beat, 9, 11)
-                run(clamp_at_two, beat, 0, 0)
-                run(make_side_hat, beat, 1, 2)
-                run(scale_centre, beat, 9, 11)
-                run(square_hats, beat, 1, 2)
-                run(keep_right, beat, 9, 11)
-                run(quantise_plane, beat, 9, 11, (CENTRE,))
-                run(keep_left, beat, 9, 11)
-                run(turn_back, beat, 8, 9)
-                run(quantise_plane, beat, 9, 11, (RIGHT,))
-                run(sort_spline, beat, -2, -2)
+                run(multiply, beat, 10, 11)
+                run(make_side_hat, beat, 2, 2)
+                run(store, beat, 12, 12)
+                run(turn_and_add_squares, beat, 3, None)
+                run(turn_back, beat, 8, None)
+                run(take_abs, beat, 1, 1)
+                run(quantise_x, beat, 9, 10)
+                run(sort_spline, beat, -1, -1)
+                run(mark_positive, beat, 9, 10)
+                run(clamp_at_one, beat, 1, 1)
+                run(scale_side, beat, 9, 10)
+                run(scale_centre, beat, 9, 10)
+                run(keep_right, beat, 9, 10)
+                run(clamp_at_two, beat, 1, 1)
+                run(quantise_plane, beat, 9, 10, (CENTRE,))
+                run(keep_left, beat, 9, 10)
+                run(quantise_weights, beat, 0, 0)
+                run(square_hats, beat, 2, 2)
                 run(prepare_base, beat, -1, -1)
                 for n in range(GRID):
                     run(prepare_spline, beat, -1, -1, (n,))
-                run(take_log, beat, 3, 5)
-                run(quantise_plane, beat, 9, 11, (LEFT,))
-                run(quantise_weights, beat, 0, 0)
-                run(add_squares, beat, 2, 4)
-                run(multiply, beat, 10, 12)
-                run(store, beat, 11, 13)
-                run(turn_and_add_squares, beat, 2, 4)
-                run(prepare_x, beat, -1, -3)
+                run(quantise_plane, beat, 9, 10, (RIGHT,))
+                run(quantise_plane, beat, 9, 10, (LEFT,))
+                run(add_squares, beat, None, 4)

@@ -42,6 +42,7 @@ HALF = 4
 
 TENSOR_SUMS = (0, 1, 2, 3)
 CODE_TILES = 2
+SIGNED = (4, 5, 6, 7)
 LAST_N_TILE = 256
 FIRST_BEAT = -2
 LAST_BEAT = 19
@@ -92,6 +93,7 @@ def tile_kanlayer_pa_kernel(tc, x, base_weight, spline_weight, out):
         turned_normaliser = {}
         is_positive = {}
         side_basis = {}
+        signed_basis = {}
         basis = {}
         quantised = {}
         sums = {}
@@ -274,9 +276,18 @@ def tile_kanlayer_pa_kernel(tc, x, base_weight, spline_weight, out):
             turned_normaliser[j] = halves
 
         def mark_positive(j):
+            if j in SIGNED:
+                return
             positive = work.tile([P, TILE_COLS], BF16)
             nc.vector.tensor_single_scalar(out=positive[:], in_=x_tile(j), scalar=0.0, op=ALU.is_gt)
             is_positive[j] = positive
+
+        def take_sign(j):
+            if j not in SIGNED:
+                return
+            sign = work.tile([P, TILE_COLS], BF16, bufs=len(SIGNED))
+            nc.scalar.activation(out=sign[:], in_=x_tile(j), func=ACT.Sign)
+            is_positive[j] = sign
 
         def scale_squares(out, square, j):
             if not turned_on_tensor(j):
@@ -301,10 +312,21 @@ def tile_kanlayer_pa_kernel(tc, x, base_weight, spline_weight, out):
             scale_squares(plane(j, CENTRE), squares[j][1], j)
 
         def keep_right(j):
-            nc.vector.tensor_tensor(out=plane(j, RIGHT), in0=side_basis[j][:], in1=is_positive[j][:], op=ALU.mult)
+            if j in SIGNED:
+                signed = work.tile([P, TILE_COLS], BF16)
+                nc.vector.tensor_tensor(out=signed[:], in0=side_basis[j][:], in1=is_positive[j][:], op=ALU.mult)
+                signed_basis[j] = signed
+            else:
+                nc.vector.tensor_tensor(out=plane(j, RIGHT), in0=side_basis[j][:], in1=is_positive[j][:], op=ALU.mult)
 
         def keep_left(j):
-            nc.vector.tensor_tensor(out=plane(j, LEFT), in0=side_basis[j][:], in1=plane(j, RIGHT), op=ALU.subtract)
+            if j in SIGNED:
+                nc.vector.tensor_single_scalar(out=plane(j, RIGHT), in_=signed_basis[j][:], scalar=0.0, op=ALU.max)
+                nc.vector.tensor_scalar(
+                    out=plane(j, LEFT), in0=signed_basis[j][:], scalar1=-1.0, scalar2=0.0, op0=ALU.mult, op1=ALU.max
+                )
+            else:
+                nc.vector.tensor_tensor(out=plane(j, LEFT), in0=side_basis[j][:], in1=plane(j, RIGHT), op=ALU.subtract)
 
         def quantise_matrix(j, m, source):
             codes, scales = quantised[j]
@@ -377,6 +399,7 @@ def tile_kanlayer_pa_kernel(tc, x, base_weight, spline_weight, out):
                 run(load_x, beat, -2, -2)
                 run(load_base, beat, -2, -2)
                 run(prepare_x, beat, -1, 0)
+                run(take_sign, beat, None, 9)
                 run(take_log, beat, 4, 6)
                 for half in range(2):
                     if beat == EXP_BEATS[half]:

@@ -42,6 +42,9 @@ HALF = 4
 
 TENSOR_SUMS = (0, 1, 2, 3)
 CODE_TILES = 2
+EARLY_TILES = 1
+EARLY_HATS = 1
+FIRST_PARTS = 2
 SIGNED = (4, 5, 6, 7)
 LAST_N_TILE = 256
 FIRST_BEAT = -2
@@ -106,7 +109,14 @@ def tile_kanlayer_pa_kernel(tc, x, base_weight, spline_weight, out):
         def load_spline(r):
             rows = slice(r * P, (r + 1) * P)
             sw_nat = loads.tile([P, FEATURES * GRID], BF16)
-            nc.sync.dma_start(out=sw_nat[:], in_=spline_weight[rows, :, :].rearrange("o i g -> o (i g)"))
+            parts = FIRST_PARTS if r == 0 else 1
+            width = FEATURES // parts
+            for part in range(parts):
+                features = slice(part * width, (part + 1) * width)
+                nc.sync.dma_start(
+                    out=sw_nat[:, part * width * GRID : (part + 1) * width * GRID],
+                    in_=spline_weight[rows, features, :].rearrange("o i g -> o (i g)"),
+                )
             natural_spline[r] = sw_nat
 
         def load_base(r):
@@ -129,14 +139,21 @@ def tile_kanlayer_pa_kernel(tc, x, base_weight, spline_weight, out):
             transpose_words(
                 natural_x[j][:].bitcast(F32),
                 x_grouped_words[:, j * words : (j + 1) * words],
-                nc.scalar.copy if j < HALF else nc.vector.tensor_copy,
+                nc.scalar.copy if j < 4 else nc.vector.tensor_copy,
             )
 
         def sort_spline(r):
             sorted_sw = prep.tile([P, GRID * FEATURES], BF16, bufs=2)
             by_grid = natural_spline[r][:].rearrange("p (i g) -> p g i", g=GRID)
-            for n, g in enumerate(GRID_ORDER):
-                nc.vector.tensor_copy(out=sorted_sw[:, n * FEATURES : (n + 1) * FEATURES], in_=by_grid[:, g, :])
+            parts = FIRST_PARTS if r == 0 else 1
+            width = FEATURES // parts
+            for part in range(parts):
+                features = slice(part * width, (part + 1) * width)
+                for n, g in enumerate(GRID_ORDER):
+                    nc.vector.tensor_copy(
+                        out=sorted_sw[:, n * FEATURES + part * width : n * FEATURES + (part + 1) * width],
+                        in_=by_grid[:, g, features],
+                    )
             sorted_spline[r] = sorted_sw
 
         def prepare_base(r):
@@ -146,7 +163,7 @@ def tile_kanlayer_pa_kernel(tc, x, base_weight, spline_weight, out):
             transpose_words(
                 natural_base[r][:].bitcast(F32),
                 w_grouped[:].bitcast(F32)[:, 0:words],
-                nc.scalar.copy if r < HALF else nc.vector.tensor_copy,
+                nc.scalar.copy if r < 3 else nc.vector.tensor_copy,
             )
 
         def prepare_spline(r, n):
@@ -394,11 +411,18 @@ def tile_kanlayer_pa_kernel(tc, x, base_weight, spline_weight, out):
                     stage(beat - offset, *args)
 
         with tc.manual_schedule():
+            for j in range(EARLY_TILES):
+                load_x(j)
             for beat in range(FIRST_BEAT, LAST_BEAT + 1):
                 run(load_spline, beat, -2, -2)
-                run(load_x, beat, -2, -2)
+                if beat + 2 >= EARLY_TILES:
+                    run(load_x, beat, -2, -2)
                 run(load_base, beat, -2, -2)
-                run(prepare_x, beat, -1, 0)
+                if beat == FIRST_BEAT:
+                    for j in range(EARLY_TILES):
+                        prepare_x(j)
+                elif beat + 1 >= EARLY_TILES:
+                    run(prepare_x, beat, -1, 0)
                 run(take_sign, beat, None, 9)
                 run(take_log, beat, 4, 6)
                 for half in range(2):
@@ -410,15 +434,21 @@ def tile_kanlayer_pa_kernel(tc, x, base_weight, spline_weight, out):
                 run(store, beat, 12, 12)
                 run(turn_and_add_squares, beat, 3, None)
                 run(turn_back, beat, 8, None)
-                run(take_abs, beat, 1, 1)
+                if beat - 1 >= EARLY_HATS:
+                    run(take_abs, beat, 1, 1)
                 run(quantise_x, beat, 9, 10)
                 run(sort_spline, beat, -1, -1)
+                if beat + 1 in range(EARLY_HATS):
+                    for stage in (take_abs, clamp_at_one, clamp_at_two):
+                        stage(beat + 1)
                 run(mark_positive, beat, 9, 10)
-                run(clamp_at_one, beat, 1, 1)
+                if beat - 1 >= EARLY_HATS:
+                    run(clamp_at_one, beat, 1, 1)
                 run(scale_side, beat, 9, 10)
                 run(scale_centre, beat, 9, 10)
                 run(keep_right, beat, 9, 10)
-                run(clamp_at_two, beat, 1, 1)
+                if beat - 1 >= EARLY_HATS:
+                    run(clamp_at_two, beat, 1, 1)
                 run(quantise_plane, beat, 9, 10, (CENTRE,))
                 run(keep_left, beat, 9, 10)
                 run(quantise_weights, beat, 0, 0)

from contextlib import ExitStack

import concourse.mybir as mybir
from concourse.masks import make_identity

BF16 = mybir.dt.bfloat16
F32 = mybir.dt.float32
U32 = mybir.dt.uint32
U8 = mybir.dt.uint8
I32 = mybir.dt.int32
FP8X4 = mybir.dt.float8_e4m3fn_x4
ACT = mybir.ActivationFunctionType
ALU = mybir.AluOpType

P = 128
PACK = 4
ROWS = 1024
FEATURES = 1024
GRID = 3
BASIS_EPS = 1e-6

ROW_TILES = ROWS // P
WORD_BLOCKS = FEATURES // 2 // P
MATRIX_PASSES = FEATURES // (P * PACK)
MATRICES = 1 + GRID
PASSES = MATRICES * MATRIX_PASSES
PASS_COLS = P * PACK
TILE_COLS = MATRIX_PASSES * PASS_COLS
N_TILE = 512
N_TILES = ROWS // N_TILE

GRID_ORDER = (1, 2, 0)
CENTRE = 0
RIGHT = 1
LEFT = 2

FLOPS = 2 * ROWS * ROWS * FEATURES * MATRICES

CLEAR_SIGNS = 0x7FFF7FFF

HALF = 4

TENSOR_SUMS = (0, 1, 2, 3)
CODE_TILES = 2
EARLY_TILES = 1
EARLY_HATS = 1
FIRST_PARTS = 2
SIGNED = (4, 5, 6, 7)
LAST_N_TILE = 256
FIRST_BEAT = -2
LAST_BEAT = 19
EXP_BEATS = (7, 13)


def tile_kanlayer_pa_kernel(tc, x, base_weight, spline_weight, out):
    nc = tc.nc
    with ExitStack() as ctx:
        consts = ctx.enter_context(tc.tile_pool(name="consts", bufs=1))
        keep = ctx.enter_context(tc.tile_pool(name="keep", bufs=1))
        loads = ctx.enter_context(tc.tile_pool(name="loads", bufs=3))
        prep = ctx.enter_context(tc.tile_pool(name="prep", bufs=1))
        work = ctx.enter_context(tc.tile_pool(name="work", bufs=1))
        psum = ctx.enter_context(tc.psum_pool(name="psum", bufs=8))

        ident = consts.tile([P, P], F32)
        make_identity(nc, ident[:])
        plus_one = consts.tile([P, P], BF16)
        nc.vector.tensor_copy(out=plus_one[:], in_=ident[:])
        minus_one = consts.tile([P, P], BF16)
        nc.vector.tensor_single_scalar(out=minus_one[:], in_=ident[:], scalar=-1.0, op=ALU.mult)
        one_col = consts.tile([P, 1], F32)
        nc.vector.memset(one_col[:], 1.0)
        eps_col = consts.tile([P, 1], F32)
        nc.vector.memset(eps_col[:], BASIS_EPS)
        first_log = consts.tile([P, 1], F32)
        nc.scalar.activation(out=first_log[:], in_=one_col[:], func=ACT.Ln)

        x_grouped = keep.tile([P, ROW_TILES * TILE_COLS], BF16, align_bytes=64)
        x_grouped_words = x_grouped[:].bitcast(F32)
        x_grouped_bits = x_grouped[:].bitcast(I32)
        w_codes = keep.tile([P, PASSES, ROWS], U32, align_bytes=64)
        w_scales = keep.tile([P, PASSES, ROWS], U8, align_bytes=64)

        natural_x = {}
        natural_base = {}
        natural_spline = {}
        sorted_spline = {}
        grouped_weights = {}
        abs_x = {}
        clamped_one = {}
        clamped_two = {}
        side_hat = {}
        squares = {}
        turned_sum = {}
        normaliser = {}
        turned_normaliser = {}
        is_positive = {}
        side_basis = {}
        signed_basis = {}
        basis = {}
        quantised = {}
        sums = {}

        def load_x(j):
            x_nat = loads.tile([P, FEATURES], BF16, bufs=2)
            nc.sync.dma_start(out=x_nat[:], in_=x[j * P : (j + 1) * P, :])
            natural_x[j] = x_nat

        def load_spline(r):
            rows = slice(r * P, (r + 1) * P)
            sw_nat = loads.tile([P, FEATURES * GRID], BF16)
            parts = FIRST_PARTS if r == 0 else 1
            width = FEATURES // parts
            for part in range(parts):
                features = slice(part * width, (part + 1) * width)
                nc.sync.dma_start(
                    out=sw_nat[:, part * width * GRID : (part + 1) * width * GRID],
                    in_=spline_weight[rows, features, :].rearrange("o i g -> o (i g)"),
                )
            natural_spline[r] = sw_nat

        def load_base(r):
            rows = slice(r * P, (r + 1) * P)
            bw_nat = loads.tile([P, FEATURES], BF16)
            nc.sync.dma_start(out=bw_nat[:], in_=base_weight[rows, :])
            natural_base[r] = bw_nat

        def transpose_words(natural_words, grouped_words, copy):
            bank = psum.tile([P, WORD_BLOCKS, P], F32, tag="bank")
            for w in range(WORD_BLOCKS):
                nc.tensor.transpose(bank[:, w, :], natural_words[:, w * P : (w + 1) * P], ident[:])
            copy(
                out=grouped_words.rearrange("p (c r u) -> p c r u", c=MATRIX_PASSES, u=2),
                in_=bank[:].rearrange("p (c u) r -> p c r u", u=2),
            )

        def prepare_x(j):
            words = TILE_COLS // 2
            transpose_words(
                natural_x[j][:].bitcast(F32),
                x_grouped_words[:, j * words : (j + 1) * words],
                nc.scalar.copy if j < 4 else nc.vector.tensor_copy,
            )

        def sort_spline(r):
            sorted_sw = prep.tile([P, GRID * FEATURES], BF16, bufs=2)
            by_grid = natural_spline[r][:].rearrange("p (i g) -> p g i", g=GRID)
            parts = FIRST_PARTS if r == 0 else 1
            width = FEATURES // parts
            for part in range(parts):
                features = slice(part * width, (part + 1) * width)
                for n, g in enumerate(GRID_ORDER):
                    nc.vector.tensor_copy(
                        out=sorted_sw[:, n * FEATURES + part * width : n * FEATURES + (part + 1) * width],
                        in_=by_grid[:, g, features],
                    )
            sorted_spline[r] = sorted_sw

        def prepare_base(r):
            w_grouped = prep.tile([P, MATRICES * TILE_COLS], BF16, bufs=2, align_bytes=64)
            grouped_weights[r] = w_grouped
            words = TILE_COLS // 2
            transpose_words(
                natural_base[r][:].bitcast(F32),
                w_grouped[:].bitcast(F32)[:, 0:words],
                nc.scalar.copy if r < 3 else nc.vector.tensor_copy,
            )

        def prepare_spline(r, n):
            w_grouped = grouped_weights[r]
            words = TILE_COLS // 2
            transpose_words(
                sorted_spline[r][:].bitcast(F32)[:, n * words : (n + 1) * words],
                w_grouped[:].bitcast(F32)[:, (1 + n) * words : (2 + n) * words],
                nc.scalar.copy,
            )

        def quantise_weights(r):
            w_grouped = grouped_weights[r]
            cols = slice(r * P, (r + 1) * P)
            for k in range(PASSES):
                nc.vector.quantize_mx(
                    out=w_codes[:, k, cols].bitcast(FP8X4),
                    scales=w_scales[:, k, cols],
                    in_=w_grouped[:, k * PASS_COLS : (k + 1) * PASS_COLS],
                )

        def x_tile(j):
            return x_grouped[:, j * TILE_COLS : (j + 1) * TILE_COLS]

        def pass_cols(c):
            return slice(c * PASS_COLS, (c + 1) * PASS_COLS)

        def take_abs(j):
            words = TILE_COLS // 2
            a = work.tile([P, TILE_COLS], BF16)
            nc.vector.tensor_single_scalar(
                out=a[:].bitcast(I32),
                in_=x_grouped_bits[:, j * words : (j + 1) * words],
                scalar=CLEAR_SIGNS,
                op=ALU.bitwise_and,
            )
            abs_x[j] = a

        def clamp_at_one(j):
            twice_min1 = work.tile([P, TILE_COLS], BF16, bufs=3)
            nc.vector.tensor_scalar(
                out=twice_min1[:], in0=abs_x[j][:], scalar1=1.0, scalar2=2.0, op0=ALU.min, op1=ALU.mult
            )
            clamped_one[j] = twice_min1

        def clamp_at_two(j):
            min2 = work.tile([P, TILE_COLS], BF16, bufs=3)
            nc.vector.tensor_single_scalar(out=min2[:], in_=abs_x[j][:], scalar=2.0, op=ALU.min)
            clamped_two[j] = min2

        def make_side_hat(j):
            halves = []
            for c in range(MATRIX_PASSES):
                side = psum.tile([P, PASS_COLS], F32, tag="bank")
                nc.tensor.matmul(
                    side[:], lhsT=plus_one[:], rhs=clamped_one[j][:, pass_cols(c)], start=True, stop=False
                )
                nc.tensor.matmul(
                    side[:], lhsT=minus_one[:], rhs=clamped_two[j][:, pass_cols(c)], start=False, stop=True
                )
                halves.append(side)
            side_hat[j] = halves

        def square_hats(j):
            r_side = work.tile([P, TILE_COLS], F32, bufs=6)
            for c in range(MATRIX_PASSES):
                nc.scalar.activation(out=r_side[:, pass_cols(c)], in_=side_hat[j][c][:], func=ACT.Square)
            r_centre = work.tile([P, TILE_COLS], F32, bufs=6)
            nc.scalar.activation(out=r_centre[:], in_=clamped_one[j][:], func=ACT.Square, scale=-0.5, bias=one_col[:])
            squares[j] = (r_side, r_centre)

        def turned_on_tensor(j):
            return j in TENSOR_SUMS

        def turn_and_add_squares(j):
            if not turned_on_tensor(j):
                return
            r_side, r_centre = squares[j]
            halves = []
            for c in range(MATRIX_PASSES):
                bank = psum.tile([P, PASS_COLS], F32, tag="bank")
                for b in range(PASS_COLS // P):
                    block = bank[:, b * P : (b + 1) * P]
                    cols = slice(c * PASS_COLS + b * P, c * PASS_COLS + (b + 1) * P)
                    nc.tensor.matmul(
                        block, lhsT=r_side[:, cols], rhs=ident[:], is_transpose=True, start=True, stop=False
                    )
                    nc.tensor.matmul(
                        block, lhsT=r_centre[:, cols], rhs=ident[:], is_transpose=True, start=False, stop=True
                    )
                halves.append(bank)
            turned_sum[j] = halves

        def add_squares(j):
            if turned_on_tensor(j):
                return
            norm = work.tile([P, TILE_COLS], F32, tag="norm", bufs=5)
            nc.vector.tensor_tensor(out=norm[:], in0=squares[j][0][:], in1=squares[j][1][:], op=ALU.add)
            normaliser[j] = norm

        def take_log(j):
            if not turned_on_tensor(j):
                norm = normaliser[j]
                nc.scalar.activation(out=norm[:], in_=norm[:], func=ACT.Ln, bias=eps_col[:])
                return
            norm = work.tile([P, TILE_COLS], F32, tag="norm", bufs=5)
            for c in range(MATRIX_PASSES):
                nc.scalar.activation(
                    out=norm[:, pass_cols(c)], in_=turned_sum[j][c][:], func=ACT.Ln, bias=eps_col[:]
                )
            normaliser[j] = norm

        def take_exp(j):
            norm = normaliser[j]
            nc.scalar.activation(out=norm[:], in_=norm[:], func=ACT.Exp, scale=-1.0)

        def turn_back(j):
            if not turned_on_tensor(j):
                return
            halves = []
            for c in range(MATRIX_PASSES):
                bank = psum.tile([P, PASS_COLS], F32, tag="bank")
                for b in range(PASS_COLS // P):
                    cols = slice(c * PASS_COLS + b * P, c * PASS_COLS + (b + 1) * P)
                    nc.tensor.transpose(bank[:, b * P : (b + 1) * P], normaliser[j][:, cols], ident[:])
                halves.append(bank)
            turned_normaliser[j] = halves

        def mark_positive(j):
            if j in SIGNED:
                return
            positive = work.tile([P, TILE_COLS], BF16)
            nc.vector.tensor_single_scalar(out=positive[:], in_=x_tile(j), scalar=0.0, op=ALU.is_gt)
            is_positive[j] = positive

        def take_sign(j):
            if j not in SIGNED:
                return
            sign = work.tile([P, TILE_COLS], BF16, bufs=len(SIGNED))
            nc.scalar.activation(out=sign[:], in_=x_tile(j), func=ACT.Sign)
            is_positive[j] = sign

        def scale_squares(out, square, j):
            if not turned_on_tensor(j):
                nc.vector.tensor_tensor(out=out, in0=square[:], in1=normaliser[j][:], op=ALU.mult)
                return
            for c in range(MATRIX_PASSES):
                nc.vector.tensor_tensor(
                    out=out[:, pass_cols(c)], in0=square[:, pass_cols(c)], in1=turned_normaliser[j][c][:], op=ALU.mult
                )

        def scale_side(j):
            b_side = work.tile([P, TILE_COLS], BF16)
            scale_squares(b_side[:], squares[j][0], j)
            side_basis[j] = b_side

        def plane(j, n):
            return basis[j][:, n * TILE_COLS : (n + 1) * TILE_COLS]

        def scale_centre(j):
            planes = work.tile([P, GRID * TILE_COLS], BF16, align_bytes=64)
            basis[j] = planes
            scale_squares(plane(j, CENTRE), squares[j][1], j)

        def keep_right(j):
            if j in SIGNED:
                signed = work.tile([P, TILE_COLS], BF16)
                nc.vector.tensor_tensor(out=signed[:], in0=side_basis[j][:], in1=is_positive[j][:], op=ALU.mult)
                signed_basis[j] = signed
            else:
                nc.vector.tensor_tensor(out=plane(j, RIGHT), in0=side_basis[j][:], in1=is_positive[j][:], op=ALU.mult)

        def keep_left(j):
            if j in SIGNED:
                nc.vector.tensor_single_scalar(out=plane(j, RIGHT), in_=signed_basis[j][:], scalar=0.0, op=ALU.max)
                nc.vector.tensor_scalar(
                    out=plane(j, LEFT), in0=signed_basis[j][:], scalar1=-1.0, scalar2=0.0, op0=ALU.mult, op1=ALU.max
                )
            else:
                nc.vector.tensor_tensor(out=plane(j, LEFT), in0=side_basis[j][:], in1=plane(j, RIGHT), op=ALU.subtract)

        def quantise_matrix(j, m, source):
            codes, scales = quantised[j]
            width = MATRIX_PASSES * P
            nc.vector.quantize_mx(
                out=codes[:, m * width : (m + 1) * width].bitcast(FP8X4),
                scales=scales[:, m * width : (m + 1) * width],
                in_=source,
            )

        def quantise_x(j):
            codes = work.tile([P, PASSES * P], U32, bufs=CODE_TILES, align_bytes=64)
            scales = work.tile([P, PASSES * P], U8, bufs=CODE_TILES, align_bytes=64)
            quantised[j] = (codes, scales)
            quantise_matrix(j, 0, x_tile(j))

        def quantise_plane(j, n):
            quantise_matrix(j, 1 + n, plane(j, n))

        def add_passes(j, passes, n):
            codes, scales = quantised[j]
            width = tile_width(j)
            cols = slice(n * width, (n + 1) * width)
            for k in passes:
                rows = slice(k * P, (k + 1) * P)
                nc.tensor.matmul_mx(
                    out=sums[j][n][:, :width],
                    lhsT=codes[:, rows].bitcast(FP8X4),
                    lhsT_scale=scales[:, rows],
                    rhs=w_codes[:, k, cols].bitcast(FP8X4),
                    rhs_scale=w_scales[:, k, cols],
                    start=(k == 0),
                    stop=(k == PASSES - 1),
                )

        def tile_width(j):
            return N_TILE if j < ROW_TILES - 1 else LAST_N_TILE

        def multiply(j):
            sums[j] = []
            tiles = range(ROWS // tile_width(j))
            for n in tiles:
                acc = psum.tile([P, N_TILE], F32, tag="bank")
                sums[j].append(acc)
            early = PASSES if j < ROW_TILES - 1 else PASSES - MATRIX_PASSES
            for k in range(early):
                for n in tiles:
                    add_passes(j, (k,), n)
            for n in tiles:
                add_passes(j, range(early, PASSES), n)

        def store(j):
            width = tile_width(j)
            for n, acc in enumerate(sums[j]):
                result = work.tile([P, N_TILE], F32, bufs=4)
                copy = nc.scalar.copy if j < ROW_TILES - 1 or n % 2 == 0 else nc.vector.tensor_copy
                copy(out=result[:, :width], in_=acc[:, :width])
                nc.sync.dma_start(
                    out=out[j * P : (j + 1) * P, n * width : (n + 1) * width], in_=result[:, :width]
                )

        def run(stage, beat, first, second, args=()):
            for half, offset in ((range(HALF), first), (range(HALF, ROW_TILES), second)):
                if offset is not None and beat - offset in half:
                    stage(beat - offset, *args)

        with tc.manual_schedule():
            for j in range(EARLY_TILES):
                load_x(j)
            for beat in range(FIRST_BEAT, LAST_BEAT + 1):
                run(load_spline, beat, -2, -2)
                if beat + 2 >= EARLY_TILES:
                    run(load_x, beat, -2, -2)
                run(load_base, beat, -2, -2)
                if beat == FIRST_BEAT:
                    for j in range(EARLY_TILES):
                        prepare_x(j)
                elif beat + 1 >= EARLY_TILES:
                    run(prepare_x, beat, -1, 0)
                run(take_sign, beat, None, 9)
                run(take_log, beat, 4, 6)
                for half in range(2):
                    if beat == EXP_BEATS[half]:
                        for j in range(half * HALF, (half + 1) * HALF):
                            take_exp(j)
                run(multiply, beat, 10, 11)
                run(make_side_hat, beat, 2, 2)
                run(store, beat, 12, 12)
                run(turn_and_add_squares, beat, 3, None)
                run(turn_back, beat, 8, None)
                if beat - 1 >= EARLY_HATS:
                    run(take_abs, beat, 1, 1)
                run(quantise_x, beat, 9, 10)
                run(sort_spline, beat, -1, -1)
                if beat + 1 in range(EARLY_HATS):
                    for stage in (take_abs, clamp_at_one, clamp_at_two):
                        stage(beat + 1)
                run(mark_positive, beat, 9, 10)
                if beat - 1 >= EARLY_HATS:
                    run(clamp_at_one, beat, 1, 1)
                run(scale_side, beat, 9, 10)
                run(scale_centre, beat, 9, 10)
                run(keep_right, beat, 9, 10)
                if beat - 1 >= EARLY_HATS:
                    run(clamp_at_two, beat, 1, 1)
                run(quantise_plane, beat, 9, 10, (CENTRE,))
                run(keep_left, beat, 9, 10)
                run(quantise_weights, beat, 0, 0)
                run(square_hats, beat, 2, 2)
                run(prepare_base, beat, -1, -1)
                for n in range(GRID):
                    run(prepare_spline, beat, -1, -1, (n,))
                run(quantise_plane, beat, 9, 10, (RIGHT,))
                run(quantise_plane, beat, 9, 10, (LEFT,))
                run(add_squares, beat, None, 4)
